import numpy as np
import ml_dtypes


def mxq(x, axis, fmt="e4m3"):
    dtype, down = {"e4m3": (ml_dtypes.float8_e4m3fn, 7), "e5m2": (ml_dtypes.float8_e5m2, 14)}[fmt]
    v = np.moveaxis(np.asarray(x, np.float32).astype(ml_dtypes.bfloat16).astype(np.float64), axis, -1)
    blocks = v.reshape(v.shape[:-1] + (-1, 32))
    amax = np.abs(blocks).max(-1, keepdims=True)
    byte = np.maximum(np.where(amax > 0, np.frexp(amax)[1] - 1 + 127, 0) - down, 1)
    scale = np.exp2(byte - 127.0)
    codes = (blocks / scale).astype(np.float32).astype(dtype).astype(np.float64)
    return np.moveaxis((codes * scale).reshape(v.shape), -1, axis)


WIDE = False


def mx_kscale(k):
    if not WIDE:
        return np.ones(k)
    levels = np.array([10, -10, 5, -5, 0])
    if k % 512:
        return np.exp2(np.random.permutation(np.resize(levels, k // 32))).repeat(32)
    a = np.empty((k // 512, 16))
    for p in range(k // 512):
        a[p, :8] = np.random.permutation(np.resize(levels, 8))
        for g in range(8):
            far = levels[np.abs(levels - a[p, g]) >= 10]
            a[p, g + 8] = far[np.random.randint(len(far))]
    return np.exp2(a.ravel()).repeat(32)


BF16 = ml_dtypes.bfloat16


def bf(x):
    return np.asarray(x, np.float32).astype(BF16)


def f64(x):
    return np.asarray(x).astype(np.float64)


B, T, C, H, D = 2, 512, 1024, 8, 128
HD = H * D
EPS = 2.0 ** -23
ROPE_BASE = 2.0 ** 10
BOUND = np.sqrt(3.0) * 0.5 / np.sqrt(C)


def rope_tables():
    freq = np.concatenate([(1.0 / ROPE_BASE) ** np.linspace(0.0, 1.0, D // 4), np.zeros(D // 4)])
    theta = f64(np.arange(T))[:, None] * freq[None, :]
    return np.cos(theta), np.sin(theta)


def apply_rope(u, cos, sin):
    u1, u2 = u[..., : D // 2], u[..., D // 2 :]
    c, s = cos[None, :, None, :], sin[None, :, None, :]
    return np.concatenate([u1 * c + u2 * s, u2 * c - u1 * s], axis=-1)


def rms_norm(u):
    return u / np.sqrt(np.mean(np.square(u), axis=-1, keepdims=True) + EPS)


def draw0():
    s = mx_kscale(C)
    return {"x": bf(np.random.standard_normal((B, T, C)) * s),
            "ve": bf(np.random.standard_normal((B, T, HD))),
            "qkv_w": bf(np.random.uniform(-BOUND, BOUND, (3, HD, C)) / s),
            "lambdas": bf(0.5 + 0.1 * np.random.standard_normal(2))}


def core(x, ve, qkv_w, lambdas):
    w = f64(qkv_w).reshape(3 * HD, C)
    qkv = (mxq(f64(x), 2, "e4m3") @ mxq(w, 1, "e4m3").T).reshape(B, T, 3, H, D)
    q, k, v = qkv[:, :, 0], qkv[:, :, 1], qkv[:, :, 2]
    cos, sin = rope_tables()
    q = apply_rope(rms_norm(q), cos, sin)
    k = apply_rope(rms_norm(k), cos, sin)
    lam = f64(lambdas)
    v = lam[0] * v + lam[1] * f64(ve).reshape(B, T, H, D)
    return q, k, v


def e4m3fn_bytes(y):
    return np.clip(np.asarray(y, np.float64), -448.0, 448.0).astype(np.float32).astype(ml_dtypes.float8_e4m3fn).view(np.uint8)


def e4m3fn_values(b):
    return np.asarray(b, np.uint8).view(ml_dtypes.float8_e4m3fn).astype(np.float64)


def setup_inputs():
    d = draw0()
    x0 = np.asarray(d['qkv_w']).astype(np.float64)
    s = (np.max(np.abs(x0), axis=(0, 1), keepdims=True) / 448.0).astype(np.float32)
    out = {}
    for k, v in d.items():
        if k == 'qkv_w':
            out['qkv_w_bytes'] = e4m3fn_bytes(x0 / s.astype(np.float64))
            out['qkv_w_scale'] = s
        else:
            out[k] = v
    return out


def reference(x, ve, qkv_w_bytes, qkv_w_scale, lambdas):
    return core(x, ve, e4m3fn_values(qkv_w_bytes) * qkv_w_scale.astype(np.float64), lambdas)

@@ -1,0 +1,352 @@
+from contextlib import ExitStack
+import math
+
+import concourse.masks as masks
+import concourse.mybir as mybir
+
+F32 = mybir.dt.float32
+BF16 = mybir.dt.bfloat16
+I32 = mybir.dt.int32
+U32 = mybir.dt.uint32
+U8 = mybir.dt.uint8
+FP8 = mybir.dt.float8_e4m3fn
+FP8X4 = mybir.dt.float8_e4m3fn_x4
+ALU = mybir.AluOpType
+ACT = mybir.ActivationFunctionType
+
+P = 128
+TOK = 1024
+C = 1024
+HEADS = 8
+D = 128
+NROT = 32
+FLOPS = 2 * TOK * C * 3 * HEADS * D
+EPS = 2.0 ** -23
+RATIO = (1.0 / 1024.0) ** (1.0 / 31.0)
+WCALLS = 32
+NHEAD = 6
+VCOPY = ()
+VNORM = (1, 5, 9, 13)
+XLAG = 3
+NBRIDGE = 6
+EV0 = 7
+
+
+def tile_causalselfattention_pa_kernel(tc, x, ve, qkv_w_bytes, qkv_w_scale, lambdas, out_0, out_1, out_2):
+    nc = tc.nc
+    xf = x.flatten_outer_dims().rearrange("(n p) k -> p n k", p=P)
+    vef = ve.flatten_outer_dims().rearrange("(n p) k -> p n k", p=P)
+    wv = qkv_w_bytes.rearrange("s n k -> (s n) k").rearrange("(c r p) k -> p c r k", r=4, p=P)
+    outs = [o.rearrange("b t h d -> (b t) (h d)") for o in (out_0, out_1, out_2)]
+
+    with ExitStack() as ctx:
+        const = ctx.enter_context(tc.tile_pool(name="const", bufs=1))
+        keep = ctx.enter_context(tc.tile_pool(name="keep", bufs=1))
+        stage = ctx.enter_context(tc.tile_pool(name="stage", bufs=2))
+        psum = ctx.enter_context(tc.psum_pool(name="psum", bufs=2))
+        ctx.enter_context(tc.manual_schedule())
+
+        scale_all = const.tile([P, C], F32, name="scale_all")
+        sc8 = const.tile([P, 8], F32, name="sc8")
+        nc.scalar.dma_start(out=sc8[:], in_=qkv_w_scale.rearrange("a b (p m) -> (a b p) m", m=8))
+        lam_bf = const.tile([P, 2], BF16, name="lam_bf")
+        nc.scalar.dma_start(out=lam_bf[:], in_=lambdas.partition_broadcast(P))
+        wbytes = [keep.tile([P, 4, C], U8, name="wbytes%d" % c) for c in range(6)]
+        xraw = [keep.tile([P, 2, C], BF16, name="xraw%d" % i) for i in range(4)]
+        veraw = [keep.tile([P, 2, C], BF16, name="veraw%d" % i) for i in range(4)]
+
+        def load_w(c):
+            nc.sync.dma_start(out=wbytes[c][:], in_=wv[:, c, :, :])
+
+        def load_x(i):
+            nc.sync.dma_start(out=xraw[i][:], in_=xf[:, 2 * i:2 * i + 2, :])
+
+        def load_ve(i):
+            nc.sync.dma_start(out=veraw[i][:], in_=vef[:, 2 * i:2 * i + 2, :])
+
+        for r in range(4):
+            nc.sync.dma_start(out=wbytes[0][:, r, :], in_=wv[:, 0, r, :])
+        load_x(0)
+        load_w(1)
+        load_x(1)
+        load_x(2)
+        load_x(3)
+        load_ve(0)
+        load_w(2)
+        load_ve(1)
+        load_w(3)
+        load_ve(2)
+        load_ve(3)
+        load_w(4)
+        load_w(5)
+
+        zeros = const.tile([P, 512], BF16, name="zeros")
+        nc.gpsimd.memset(zeros[:], 0.0)
+        tpos = const.tile([P, 4], F32, name="tpos")
+        nc.gpsimd.iota(tpos[:], pattern=[[P, 4]], base=0, channel_multiplier=1, allow_small_or_imprecise_dtypes=True)
+        ident = const.tile([P, P], F32, name="ident")
+        masks.make_identity(nc, ident[:])
+        eps = const.tile([P, 1], F32, name="eps")
+        nc.vector.memset(eps[:], EPS)
+        turns = const.tile([P, 2, 4, NROT], F32, name="turns")
+        nc.vector.tensor_scalar(out=turns[:, 0, :, 0], in0=tpos[:], scalar1=1.0 / (2.0 * math.pi), scalar2=None, op0=ALU.mult)
+        for n in (1, 2, 4, 8, 16):
+            nc.vector.tensor_scalar(out=turns[:, 0, :, n:2 * n], in0=turns[:, 0, :, 0:n], scalar1=RATIO ** n, scalar2=None, op0=ALU.mult)
+        nc.vector.tensor_scalar(out=turns[:, 1, :, :], in0=turns[:, 0, :, :], scalar1=0.25, scalar2=None, op0=ALU.add)
+        turns_flat = turns[:].rearrange("p a j i -> p (a j i)")
+        whole_i = const.tile([P, 8 * NROT], I32, name="whole_i")
+        nc.vector.tensor_copy(out=whole_i[:], in_=turns_flat)
+        whole_f = const.tile([P, 8 * NROT], F32, name="whole_f")
+        nc.vector.tensor_copy(out=whole_f[:], in_=whole_i[:])
+        frac = const.tile([P, 8 * NROT], F32, name="frac")
+        nc.vector.tensor_tensor(out=frac[:], in0=turns_flat, in1=whole_f[:], op=ALU.subtract)
+        negfrac = const.tile([P, 8 * NROT], F32, name="negfrac")
+        nc.vector.scalar_tensor_tensor(out=negfrac[:], in0=frac[:], scalar=0.5, in1=frac[:], op0=ALU.is_gt, op1=ALU.subtract)
+        tab = const.tile([P, 2, 4, NROT], F32, name="tab")
+        nc.scalar.activation(out=tab[:].rearrange("p a j i -> p (a j i)"), in_=negfrac[:], func=ACT.Sin, scale=-2.0 * math.pi)
+        lam = const.tile([P, 2], F32, name="lam")
+        nc.vector.tensor_copy(out=lam[:], in_=lam_bf[:])
+
+        xc = [keep.tile([P, 256], U32, name="xc%d" % i, align_bytes=64) for i in range(8)]
+        xs = [keep.tile([P, 256], U8, name="xs%d" % i, align_bytes=64) for i in range(8)]
+        wc = [keep.tile([P, 1024], U32, name="wc%d" % c, align_bytes=64) for c in range(6)]
+        ws = [keep.tile([P, 1024], U8, name="ws%d" % c, align_bytes=64) for c in range(6)]
+        ve1 = [keep.tile([P, C], F32, name="ve1_%d" % i) for i in range(8)]
+        st = {}
+
+        def idle_matmuls(n):
+            warmbank = psum.tile([P, 512], F32, name="tp", tag="tp", bufs=2)
+            for k in range(n):
+                nc.tensor.matmul(out=warmbank[:], lhsT=zeros[:, 0:P], rhs=zeros[:], start=True, stop=True)
+
+        idle_matmuls(4)
+        warm = const.tile([P, 1], F32, name="warm")
+        nc.scalar.activation(out=warm[:], in_=eps[:], func=ACT.Abs_reciprocal_sqrt)
+
+        for half in range(2):
+            sbank = psum.tile([P, 4, P], F32, name="tp", tag="tp", bufs=2)
+            for mm in range(4):
+                nc.tensor.transpose(sbank[:, mm, :], sc8[:, 4 * half + mm:4 * half + mm + 1].to_broadcast([P, P]), ident[:])
+            mover = nc.vector.tensor_copy if half == 0 else nc.scalar.copy
+            mover(out=scale_all[:].rearrange("p (n m) -> p n m", m=8)[:, :, 4 * half:4 * half + 4],
+                  in_=sbank[:].rearrange("p m n -> p n m"))
+        idle_matmuls(NHEAD - 4)
+
+        def transposes(key, words):
+            tp = psum.tile([P, 2, 2, P], F32, name="tp", tag="tp", bufs=2)
+            st["calls"] = st.get("calls", 0) + 1
+            if st["calls"] <= WCALLS:
+                nc.tensor.matmul(out=tp[:].rearrange("p g u r -> p (g u r)"), lhsT=zeros[:, 0:P], rhs=zeros[:], start=True, stop=True)
+            for g in range(2):
+                for u in range(2):
+                    nc.tensor.transpose(tp[:, g, u, :], words[:, 256 * g + u:256 * (g + 1):2], ident[:])
+            st[key] = tp
+
+        def x_transpose(i):
+            transposes(("xt", i), xraw[i // 2][:, i % 2, :].bitcast(F32))
+
+        def x_copy(i):
+            xg = stage.tile([P, 2, P, 2], F32, name="xg", tag="xg", bufs=5, align_bytes=64)
+            nc.scalar.copy(out=xg[:], in_=st["xt", i][:].rearrange("p g u r -> p g r u"))
+            st["xg", i] = xg
+
+        def x_quant(i):
+            nc.vector.quantize_mx(out=xc[i][:].bitcast(FP8X4), scales=xs[i][:],
+                                  in_=st["xg", i][:].rearrange("p g r u -> p (g r u)").bitcast(BF16))
+
+        def w_widen(rt):
+            wb = stage.tile([P, C], BF16, name="wb", tag="wb", bufs=6)
+            nc.vector.tensor_tensor(out=wb[:], in0=wbytes[rt // 4][:, rt % 4, :].bitcast(FP8), in1=scale_all[:], op=ALU.mult)
+            st["wb", rt] = wb
+
+        def w_transpose(rt):
+            transposes(("wt", rt), st["wb", rt][:].bitcast(F32))
+
+        def w_copy(rt):
+            c, r = divmod(rt, 4)
+            if r == 0:
+                st["wg", c] = stage.tile([P, 2, 512, 2], F32, name="wg", tag="wg", bufs=2, align_bytes=64)
+            mover = nc.vector.tensor_copy if rt in VCOPY else nc.scalar.copy
+            mover(out=st["wg", c][:, :, r * P:(r + 1) * P, :], in_=st["wt", rt][:].rearrange("p g u r -> p g r u"))
+
+        def w_quant(c):
+            nc.vector.quantize_mx(out=wc[c][:].bitcast(FP8X4), scales=ws[c][:],
+                                  in_=st["wg", c][:].rearrange("p g r u -> p (g r u)").bitcast(BF16))
+
+        def project(key, tt, sec, tag, bufs):
+            banks = []
+            for half in range(2):
+                acc = psum.tile([P, 512], F32, name=tag, tag=tag, bufs=bufs)
+                c = 2 * sec + half
+                for g in range(2):
+                    nc.tensor.matmul_mx(out=acc[:],
+                                        lhsT=xc[tt][:, g * P:(g + 1) * P].bitcast(FP8X4),
+                                        lhsT_scale=xs[tt][:, g * P:(g + 1) * P],
+                                        rhs=wc[c][:, g * 512:(g + 1) * 512].bitcast(FP8X4),
+                                        rhs_scale=ws[c][:, g * 512:(g + 1) * 512],
+                                        start=(g == 0), stop=(g == 1))
+                banks.append(acc)
+            st[key] = banks
+
+        def matmuls(u):
+            project(("acc", u), u % 8, u // 8, "acc", 6)
+
+        def head_cols(u, h):
+            return st["acc", u][h // 4][:, (h % 4) * D:(h % 4 + 1) * D]
+
+        def squares(u):
+            ss = stage.tile([P, HEADS], F32, name="ss", tag="ss", bufs=4)
+            for h in range(HEADS):
+                junk = stage.tile([P, D], F32, name="junk", tag="junk", bufs=8)
+                nc.scalar.activation(out=junk[:], in_=head_cols(u, h), func=ACT.Square, accum_out=ss[:, h:h + 1])
+            st["ss", u] = ss
+
+        def root(u):
+            rinv = stage.tile([P, HEADS], F32, name="rinv", tag="rinv", bufs=4)
+            nc.scalar.activation(out=rinv[:], in_=st["ss", u][:], func=ACT.Abs_reciprocal_sqrt, bias=eps[:, 0:1], scale=1.0 / D)
+            st["rinv", u] = rinv
+
+        def recip(u):
+            return
+
+        def normalise(u):
+            o = stage.tile([P, HEADS * D], F32, name="o", tag="o", bufs=6)
+            st["o", u] = o
+            if u in VNORM:
+                for b in range(2):
+                    nc.vector.tensor_tensor(out=o[:, b * 512:(b + 1) * 512].rearrange("p (h d) -> p h d", d=D),
+                                            in0=st["acc", u][b][:].rearrange("p (h d) -> p h d", d=D),
+                                            in1=st["rinv", u][:, 4 * b:4 * b + 4].unsqueeze(2).to_broadcast([P, 4, D]), op=ALU.mult)
+                return
+            for h in range(HEADS):
+                nc.scalar.activation(out=o[:, h * D:(h + 1) * D], in_=head_cols(u, h), func=ACT.Copy,
+                                     scale=st["rinv", u][:, h:h + 1])
+            st["o", u] = o
+
+        def rope_mul(u, h0=0, nh=HEADS):
+            j = u % 4
+            rot = st["o", u][:, h0 * D:(h0 + nh) * D].rearrange("p (m d) -> p m d", d=64)[:, :, 0:NROT]
+            ra = stage.tile([P, 2 * nh, NROT], F32, name="ra", tag="ra", bufs=2)
+            rb = stage.tile([P, 2 * nh, NROT], F32, name="rb", tag="rb", bufs=2)
+            nc.vector.tensor_tensor(out=ra[:], in0=rot, in1=tab[:, 1, j, :].unsqueeze(1).to_broadcast([P, 2 * nh, NROT]), op=ALU.mult)
+            nc.vector.tensor_tensor(out=rb[:], in0=rot, in1=tab[:, 0, j, :].unsqueeze(1).to_broadcast([P, 2 * nh, NROT]), op=ALU.mult)
+            st["ra", u, h0] = ra
+            st["rb", u, h0] = rb
+
+        def rope_add(u, h0=0, nh=HEADS):
+            cols = slice(h0 * D, (h0 + nh) * D)
+            o4 = st["o", u][:, cols].rearrange("p (h w d) -> p h w d", w=2, d=64)
+            a4 = st["ra", u, h0][:].rearrange("p (h w) i -> p h w i", w=2)
+            b4 = st["rb", u, h0][:].rearrange("p (h w) i -> p h w i", w=2)
+            nc.vector.tensor_tensor(out=o4[:, :, 0, 0:NROT], in0=a4[:, :, 0, :], in1=b4[:, :, 1, :], op=ALU.add)
+            nc.vector.tensor_tensor(out=o4[:, :, 1, 0:NROT], in0=a4[:, :, 1, :], in1=b4[:, :, 0, :], op=ALU.subtract)
+            tt = u % 8
+            nc.sync.dma_start(out=outs[u // 8][tt * P:(tt + 1) * P, cols], in_=st["o", u][:, cols])
+
+        def ve_scale(tt):
+            nc.scalar.activation(out=ve1[tt][:], in_=veraw[tt // 2][:, tt % 2, :], func=ACT.Copy, scale=lam[:, 1:2])
+
+        def value_matmuls(tt):
+            project(("accv", tt), tt, 2, "tp", 2)
+
+        def value_blend(tt, half):
+            if half == 0:
+                st["ov", tt] = stage.tile([P, HEADS * D], F32, name="o", tag="o", bufs=6)
+            cols = slice(half * 512, (half + 1) * 512)
+            nc.vector.scalar_tensor_tensor(out=st["ov", tt][:, cols], in0=st["accv", tt][half][:], scalar=lam[:, 0:1],
+                                           in1=ve1[tt][:, cols], op0=ALU.mult, op1=ALU.add)
+            nc.sync.dma_start(out=outs[2][tt * P:(tt + 1) * P, cols], in_=st["ov", tt][:, cols])
+
+        q = {"w": 0, "c": 0, "z": 0, "xq": 0, "ve": 0}
+
+        def widen(n):
+            for k in range(n):
+                if q["w"] < 24:
+                    w_widen(q["w"])
+                    w_transpose(q["w"])
+                    q["w"] += 1
+
+        def copy(n):
+            for k in range(n):
+                if q["c"] < q["w"]:
+                    w_copy(q["c"])
+                    q["c"] += 1
+
+        def quant():
+            if q["z"] < 6 and q["c"] >= 4 * q["z"] + 4:
+                w_quant(q["z"])
+                q["z"] += 1
+
+        def xquant(upto):
+            while q["xq"] <= upto:
+                x_quant(q["xq"])
+                q["xq"] += 1
+
+        def vescale(n):
+            for k in range(n):
+                if q["ve"] < 8:
+                    ve_scale(q["ve"])
+                    q["ve"] += 1
+
+        def x_turn(i):
+            x_transpose(i)
+            x_copy(i)
+
+        for i in range(8):
+            x_turn(i)
+            widen(1)
+            copy(1)
+            xquant(i - XLAG)
+            if i == 6:
+                quant()
+            if i >= 6:
+                vescale(1)
+        widen(2)
+        xquant(7)
+        quant()
+        copy(1)
+        matmuls(0)
+        vescale(1)
+        copy(1)
+        matmuls(1)
+        vescale(1)
+        squares(0)
+        widen(1)
+        copy(1)
+        root(0)
+        widen(NBRIDGE - 3)
+        recip(0)
+
+        for t in range(17):
+            if t + 2 <= 15:
+                matmuls(t + 2)
+            if t + 1 <= 15:
+                squares(t + 1)
+            copy(1)
+            if t + 1 <= 15:
+                root(t + 1)
+            if 1 <= t <= 15:
+                rope_mul(t - 1)
+            if t == 16:
+                rope_mul(15, 0, 4)
+                rope_mul(15, 4, 4)
+                rope_add(15, 0, 4)
+                rope_add(15, 4, 4)
+            widen(1)
+            if EV0 <= t <= EV0 + 7:
+                value_blend(t - EV0, 0)
+            if t <= 15:
+                normalise(t)
+            if 1 <= t <= 15:
+                rope_add(t - 1)
+            copy(1)
+            widen(1)
+            quant()
+            if EV0 <= t <= EV0 + 7:
+                value_blend(t - EV0, 1)
+            if t + 1 <= 15:
+                recip(t + 1)
+            if EV0 - 1 <= t <= EV0 + 6:
+                value_matmuls(t - EV0 + 1)
+            if t <= 3:
+                vescale(1)

@@ -23,8 +23,6 @@ NROT = 32
 FLOPS = 2 * TOK * C * 3 * HEADS * D
 EPS = 2.0 ** -23
 RATIO = (1.0 / 1024.0) ** (1.0 / 31.0)
-WCALLS = 32
-NHEAD = 6
 VCOPY = ()
 VNORM = (1, 5, 9, 13)
 XLAG = 3
@@ -80,8 +78,6 @@ def tile_causalselfattention_pa_kernel(tc, x, ve, qkv_w_bytes, qkv_w_scale, lamb
         load_w(4)
         load_w(5)
 
-        zeros = const.tile([P, 512], BF16, name="zeros")
-        nc.gpsimd.memset(zeros[:], 0.0)
         tpos = const.tile([P, 4], F32, name="tpos")
         nc.gpsimd.iota(tpos[:], pattern=[[P, 4]], base=0, channel_multiplier=1, allow_small_or_imprecise_dtypes=True)
         ident = const.tile([P, P], F32, name="ident")
@@ -114,12 +110,6 @@ def tile_causalselfattention_pa_kernel(tc, x, ve, qkv_w_bytes, qkv_w_scale, lamb
         ve1 = [keep.tile([P, C], F32, name="ve1_%d" % i) for i in range(8)]
         st = {}
 
-        def idle_matmuls(n):
-            warmbank = psum.tile([P, 512], F32, name="tp", tag="tp", bufs=2)
-            for k in range(n):
-                nc.tensor.matmul(out=warmbank[:], lhsT=zeros[:, 0:P], rhs=zeros[:], start=True, stop=True)
-
-        idle_matmuls(4)
         warm = const.tile([P, 1], F32, name="warm")
         nc.scalar.activation(out=warm[:], in_=eps[:], func=ACT.Abs_reciprocal_sqrt)
 
@@ -130,13 +120,9 @@ def tile_causalselfattention_pa_kernel(tc, x, ve, qkv_w_bytes, qkv_w_scale, lamb
             mover = nc.vector.tensor_copy if half == 0 else nc.scalar.copy
             mover(out=scale_all[:].rearrange("p (n m) -> p n m", m=8)[:, :, 4 * half:4 * half + 4],
                   in_=sbank[:].rearrange("p m n -> p n m"))
-        idle_matmuls(NHEAD - 4)
 
         def transposes(key, words):
             tp = psum.tile([P, 2, 2, P], F32, name="tp", tag="tp", bufs=2)
-            st["calls"] = st.get("calls", 0) + 1
-            if st["calls"] <= WCALLS:
-                nc.tensor.matmul(out=tp[:].rearrange("p g u r -> p (g u r)"), lhsT=zeros[:, 0:P], rhs=zeros[:], start=True, stop=True)
             for g in range(2):
                 for u in range(2):
                     nc.tensor.transpose(tp[:, g, u, :], words[:, 256 * g + u:256 * (g + 1):2], ident[:])

@@ -182,9 +182,10 @@ def tile_causalselfattention_pa_kernel(tc, x, ve, qkv_w_bytes, qkv_w_scale, lamb
 
         def squares(u):
             ss = stage.tile([P, HEADS], F32, name="ss", tag="ss", bufs=4)
+            o = stage.tile([P, HEADS * D], F32, name="o", tag="o", bufs=6)
+            st["o", u] = o
             for h in range(HEADS):
-                junk = stage.tile([P, D], F32, name="junk", tag="junk", bufs=8)
-                nc.scalar.activation(out=junk[:], in_=head_cols(u, h), func=ACT.Square, accum_out=ss[:, h:h + 1])
+                nc.scalar.activation(out=o[:, h * D:(h + 1) * D], in_=head_cols(u, h), func=ACT.Square, accum_out=ss[:, h:h + 1])
             st["ss", u] = ss
 
         def root(u):
@@ -196,8 +197,7 @@ def tile_causalselfattention_pa_kernel(tc, x, ve, qkv_w_bytes, qkv_w_scale, lamb
             return
 
         def normalise(u):
-            o = stage.tile([P, HEADS * D], F32, name="o", tag="o", bufs=6)
-            st["o", u] = o
+            o = st["o", u]
             if u in VNORM:
                 for b in range(2):
                     nc.vector.tensor_tensor(out=o[:, b * 512:(b + 1) * 512].rearrange("p (h d) -> p h d", d=D),
@@ -207,7 +207,6 @@ def tile_causalselfattention_pa_kernel(tc, x, ve, qkv_w_bytes, qkv_w_scale, lamb
             for h in range(HEADS):
                 nc.scalar.activation(out=o[:, h * D:(h + 1) * D], in_=head_cols(u, h), func=ACT.Copy,
                                      scale=st["rinv", u][:, h:h + 1])
-            st["o", u] = o
 
         def rope_mul(u, h0=0, nh=HEADS):
             j = u % 4
@@ -237,7 +236,7 @@ def tile_causalselfattention_pa_kernel(tc, x, ve, qkv_w_bytes, qkv_w_scale, lamb
 
         def value_blend(tt, half):
             if half == 0:
-                st["ov", tt] = stage.tile([P, HEADS * D], F32, name="o", tag="o", bufs=6)
+                st["ov", tt] = stage.tile([P, HEADS * D], F32, name="ov", tag="ov", bufs=3)
             cols = slice(half * 512, (half + 1) * 512)
             nc.vector.scalar_tensor_tensor(out=st["ov", tt][:, cols], in0=st["accv", tt][half][:], scalar=lam[:, 0:1],
                                            in1=ve1[tt][:, cols], op0=ALU.mult, op1=ALU.add)

@@ -24,7 +24,7 @@ FLOPS = 2 * TOK * C * 3 * HEADS * D
 EPS = 2.0 ** -23
 RATIO = (1.0 / 1024.0) ** (1.0 / 31.0)
 VCOPY = ()
-VNORM = (1, 5, 9, 13)
+VNORM = (1, 3, 5)
 XLAG = 3
 NBRIDGE = 6
 EV0 = 7

@@ -28,6 +28,7 @@ VNORM = (1, 3, 5)
 XLAG = 3
 NBRIDGE = 6
 EV0 = 7
+HEADRUNS = 18
 
 
 def tile_causalselfattention_pa_kernel(tc, x, ve, qkv_w_bytes, qkv_w_scale, lambdas, out_0, out_1, out_2):
@@ -62,14 +63,17 @@ def tile_causalselfattention_pa_kernel(tc, x, ve, qkv_w_bytes, qkv_w_scale, lamb
         def load_ve(i):
             nc.sync.dma_start(out=veraw[i][:], in_=vef[:, 2 * i:2 * i + 2, :])
 
-        for r in range(4):
+        for r in range(2):
+            nc.sync.dma_start(out=veraw[0][:, r, :], in_=vef[:, r, :])
+        nc.sync.dma_start(out=xraw[0][:, 0, :], in_=xf[:, 0, :])
+        nc.sync.dma_start(out=wbytes[0][:, 0, :], in_=wv[:, 0, 0, :])
+        nc.sync.dma_start(out=xraw[0][:, 1, :], in_=xf[:, 1, :])
+        for r in range(1, 4):
             nc.sync.dma_start(out=wbytes[0][:, r, :], in_=wv[:, 0, r, :])
-        load_x(0)
         load_w(1)
         load_x(1)
         load_x(2)
         load_x(3)
-        load_ve(0)
         load_w(2)
         load_ve(1)
         load_w(3)
@@ -113,6 +117,8 @@ def tile_causalselfattention_pa_kernel(tc, x, ve, qkv_w_bytes, qkv_w_scale, lamb
         warm = const.tile([P, 1], F32, name="warm")
         nc.scalar.activation(out=warm[:], in_=eps[:], func=ACT.Abs_reciprocal_sqrt)
 
+        nc.scalar.activation(out=ve1[0][:], in_=veraw[0][:, 0, :], func=ACT.Copy, scale=lam[:, 1:2])
+
         for half in range(2):
             sbank = psum.tile([P, 4, P], F32, name="tp", tag="tp", bufs=2)
             for mm in range(4):
@@ -120,9 +126,14 @@ def tile_causalselfattention_pa_kernel(tc, x, ve, qkv_w_bytes, qkv_w_scale, lamb
             mover = nc.vector.tensor_copy if half == 0 else nc.scalar.copy
             mover(out=scale_all[:].rearrange("p (n m) -> p n m", m=8)[:, :, 4 * half:4 * half + 4],
                   in_=sbank[:].rearrange("p m n -> p n m"))
+        nc.vector.tensor_scalar(out=ve1[1][:], in0=veraw[0][:, 1, :], scalar1=lam[:, 1:2], scalar2=None, op0=ALU.mult)
 
         def transposes(key, words):
-            tp = psum.tile([P, 2, 2, P], F32, name="tp", tag="tp", bufs=2)
+            st["runs"] = st.get("runs", 0) + 1
+            if st["runs"] <= HEADRUNS and st["runs"] % 4 != 0:
+                tp = psum.tile([P, 2, 2, P], F32, name="acc", tag="acc", bufs=6)
+            else:
+                tp = psum.tile([P, 2, 2, P], F32, name="tp", tag="tp", bufs=2)
             for g in range(2):
                 for u in range(2):
                     nc.tensor.transpose(tp[:, g, u, :], words[:, 256 * g + u:256 * (g + 1):2], ident[:])
@@ -242,7 +253,7 @@ def tile_causalselfattention_pa_kernel(tc, x, ve, qkv_w_bytes, qkv_w_scale, lamb
                                            in1=ve1[tt][:, cols], op0=ALU.mult, op1=ALU.add)
             nc.sync.dma_start(out=outs[2][tt * P:(tt + 1) * P, cols], in_=st["ov", tt][:, cols])
 
-        q = {"w": 0, "c": 0, "z": 0, "xq": 0, "ve": 0}
+        q = {"w": 0, "c": 0, "z": 0, "xq": 0, "ve": 2}
 
         def widen(n):
             for k in range(n):

@@ -63,8 +63,7 @@ def tile_causalselfattention_pa_kernel(tc, x, ve, qkv_w_bytes, qkv_w_scale, lamb
         def load_ve(i):
             nc.sync.dma_start(out=veraw[i][:], in_=vef[:, 2 * i:2 * i + 2, :])
 
-        for r in range(2):
-            nc.sync.dma_start(out=veraw[0][:, r, :], in_=vef[:, r, :])
+        nc.sync.dma_start(out=veraw[0][:, 0, :], in_=vef[:, 0, :])
         nc.sync.dma_start(out=xraw[0][:, 0, :], in_=xf[:, 0, :])
         nc.sync.dma_start(out=wbytes[0][:, 0, :], in_=wv[:, 0, 0, :])
         nc.sync.dma_start(out=xraw[0][:, 1, :], in_=xf[:, 1, :])
@@ -74,6 +73,7 @@ def tile_causalselfattention_pa_kernel(tc, x, ve, qkv_w_bytes, qkv_w_scale, lamb
         load_x(1)
         load_x(2)
         load_x(3)
+        nc.sync.dma_start(out=veraw[0][:, 1, :], in_=vef[:, 1, :])
         load_w(2)
         load_ve(1)
         load_w(3)
@@ -123,10 +123,8 @@ def tile_causalselfattention_pa_kernel(tc, x, ve, qkv_w_bytes, qkv_w_scale, lamb
             sbank = psum.tile([P, 4, P], F32, name="tp", tag="tp", bufs=2)
             for mm in range(4):
                 nc.tensor.transpose(sbank[:, mm, :], sc8[:, 4 * half + mm:4 * half + mm + 1].to_broadcast([P, P]), ident[:])
-            mover = nc.vector.tensor_copy if half == 0 else nc.scalar.copy
-            mover(out=scale_all[:].rearrange("p (n m) -> p n m", m=8)[:, :, 4 * half:4 * half + 4],
-                  in_=sbank[:].rearrange("p m n -> p n m"))
-        nc.vector.tensor_scalar(out=ve1[1][:], in0=veraw[0][:, 1, :], scalar1=lam[:, 1:2], scalar2=None, op0=ALU.mult)
+            nc.vector.tensor_copy(out=scale_all[:].rearrange("p (n m) -> p n m", m=8)[:, :, 4 * half:4 * half + 4],
+                                  in_=sbank[:].rearrange("p m n -> p n m"))
 
         def transposes(key, words):
             st["runs"] = st.get("runs", 0) + 1
@@ -253,7 +251,7 @@ def tile_causalselfattention_pa_kernel(tc, x, ve, qkv_w_bytes, qkv_w_scale, lamb
                                            in1=ve1[tt][:, cols], op0=ALU.mult, op1=ALU.add)
             nc.sync.dma_start(out=outs[2][tt * P:(tt + 1) * P, cols], in_=st["ov", tt][:, cols])
 
-        q = {"w": 0, "c": 0, "z": 0, "xq": 0, "ve": 2}
+        q = {"w": 0, "c": 0, "z": 0, "xq": 0, "ve": 1}
 
         def widen(n):
             for k in range(n):

@@ -29,6 +29,7 @@ XLAG = 3
 NBRIDGE = 6
 EV0 = 7
 HEADRUNS = 18
+NWARM = 4
 
 
 def tile_causalselfattention_pa_kernel(tc, x, ve, qkv_w_bytes, qkv_w_scale, lambdas, out_0, out_1, out_2):
@@ -82,12 +83,14 @@ def tile_causalselfattention_pa_kernel(tc, x, ve, qkv_w_bytes, qkv_w_scale, lamb
         load_w(4)
         load_w(5)
 
+        zeros = const.tile([P, 512], BF16, name="zeros")
+        nc.vector.memset(zeros[:], 0.0)
         tpos = const.tile([P, 4], F32, name="tpos")
         nc.gpsimd.iota(tpos[:], pattern=[[P, 4]], base=0, channel_multiplier=1, allow_small_or_imprecise_dtypes=True)
         ident = const.tile([P, P], F32, name="ident")
         masks.make_identity(nc, ident[:])
         eps = const.tile([P, 1], F32, name="eps")
-        nc.vector.memset(eps[:], EPS)
+        nc.gpsimd.memset(eps[:], EPS)
         turns = const.tile([P, 2, 4, NROT], F32, name="turns")
         nc.vector.tensor_scalar(out=turns[:, 0, :, 0], in0=tpos[:], scalar1=1.0 / (2.0 * math.pi), scalar2=None, op0=ALU.mult)
         for n in (1, 2, 4, 8, 16):
@@ -96,16 +99,14 @@ def tile_causalselfattention_pa_kernel(tc, x, ve, qkv_w_bytes, qkv_w_scale, lamb
         turns_flat = turns[:].rearrange("p a j i -> p (a j i)")
         whole_i = const.tile([P, 8 * NROT], I32, name="whole_i")
         nc.vector.tensor_copy(out=whole_i[:], in_=turns_flat)
-        whole_f = const.tile([P, 8 * NROT], F32, name="whole_f")
-        nc.vector.tensor_copy(out=whole_f[:], in_=whole_i[:])
         frac = const.tile([P, 8 * NROT], F32, name="frac")
-        nc.vector.tensor_tensor(out=frac[:], in0=turns_flat, in1=whole_f[:], op=ALU.subtract)
+        nc.vector.tensor_tensor(out=frac[:], in0=turns_flat, in1=whole_i[:], op=ALU.subtract)
         negfrac = const.tile([P, 8 * NROT], F32, name="negfrac")
         nc.vector.scalar_tensor_tensor(out=negfrac[:], in0=frac[:], scalar=0.5, in1=frac[:], op0=ALU.is_gt, op1=ALU.subtract)
         tab = const.tile([P, 2, 4, NROT], F32, name="tab")
         nc.scalar.activation(out=tab[:].rearrange("p a j i -> p (a j i)"), in_=negfrac[:], func=ACT.Sin, scale=-2.0 * math.pi)
         lam = const.tile([P, 2], F32, name="lam")
-        nc.vector.tensor_copy(out=lam[:], in_=lam_bf[:])
+        nc.gpsimd.tensor_copy(out=lam[:], in_=lam_bf[:])
 
         xc = [keep.tile([P, 256], U32, name="xc%d" % i, align_bytes=64) for i in range(8)]
         xs = [keep.tile([P, 256], U8, name="xs%d" % i, align_bytes=64) for i in range(8)]
@@ -114,6 +115,9 @@ def tile_causalselfattention_pa_kernel(tc, x, ve, qkv_w_bytes, qkv_w_scale, lamb
         ve1 = [keep.tile([P, C], F32, name="ve1_%d" % i) for i in range(8)]
         st = {}
 
+        warmbank = psum.tile([P, 512], F32, name="tp", tag="tp", bufs=2)
+        for k in range(NWARM):
+            nc.tensor.matmul(out=warmbank[:], lhsT=zeros[:, 0:P], rhs=zeros[:], start=True, stop=True)
         warm = const.tile([P, 1], F32, name="warm")
         nc.scalar.activation(out=warm[:], in_=eps[:], func=ACT.Abs_reciprocal_sqrt)
 

@@ -23,13 +23,12 @@ NROT = 32
 FLOPS = 2 * TOK * C * 3 * HEADS * D
 EPS = 2.0 ** -23
 RATIO = (1.0 / 1024.0) ** (1.0 / 31.0)
-VCOPY = ()
-VNORM = (1, 3, 5)
-XLAG = 3
-NBRIDGE = 6
-EV0 = 7
-HEADRUNS = 18
+HEADRUNS = 12
 NWARM = 4
+VADD = (9, 11, 13, 15)
+V0 = 8
+VCAST = (0, 1)
+SCAST = (4, 6, 8, 11, 14, 17, 20, 23)
 
 
 def tile_causalselfattention_pa_kernel(tc, x, ve, qkv_w_bytes, qkv_w_scale, lambdas, out_0, out_1, out_2):
@@ -37,7 +36,7 @@ def tile_causalselfattention_pa_kernel(tc, x, ve, qkv_w_bytes, qkv_w_scale, lamb
     xf = x.flatten_outer_dims().rearrange("(n p) k -> p n k", p=P)
     vef = ve.flatten_outer_dims().rearrange("(n p) k -> p n k", p=P)
     wv = qkv_w_bytes.rearrange("s n k -> (s n) k").rearrange("(c r p) k -> p c r k", r=4, p=P)
-    outs = [o.rearrange("b t h d -> (b t) (h d)") for o in (out_0, out_1, out_2)]
+    outs = [o.rearrange("b t h d -> (b t) (h d)").rearrange("(n p) c -> p n c", p=P) for o in (out_0, out_1, out_2)]
 
     with ExitStack() as ctx:
         const = ctx.enter_context(tc.tile_pool(name="const", bufs=1))
@@ -46,9 +45,8 @@ def tile_causalselfattention_pa_kernel(tc, x, ve, qkv_w_bytes, qkv_w_scale, lamb
         psum = ctx.enter_context(tc.psum_pool(name="psum", bufs=2))
         ctx.enter_context(tc.manual_schedule())
 
-        scale_all = const.tile([P, C], F32, name="scale_all")
-        sc8 = const.tile([P, 8], F32, name="sc8")
-        nc.scalar.dma_start(out=sc8[:], in_=qkv_w_scale.rearrange("a b (p m) -> (a b p) m", m=8))
+        sck = const.tile([P, 2, 4], F32, name="sck")
+        nc.scalar.dma_start(out=sck[:], in_=qkv_w_scale.rearrange("a b (g p t) -> p (a b g) t", p=P, t=4))
         lam_bf = const.tile([P, 2], BF16, name="lam_bf")
         nc.scalar.dma_start(out=lam_bf[:], in_=lambdas.partition_broadcast(P))
         wbytes = [keep.tile([P, 4, C], U8, name="wbytes%d" % c) for c in range(6)]
@@ -64,23 +62,22 @@ def tile_causalselfattention_pa_kernel(tc, x, ve, qkv_w_bytes, qkv_w_scale, lamb
         def load_ve(i):
             nc.sync.dma_start(out=veraw[i][:], in_=vef[:, 2 * i:2 * i + 2, :])
 
-        nc.sync.dma_start(out=veraw[0][:, 0, :], in_=vef[:, 0, :])
-        nc.sync.dma_start(out=xraw[0][:, 0, :], in_=xf[:, 0, :])
         nc.sync.dma_start(out=wbytes[0][:, 0, :], in_=wv[:, 0, 0, :])
+        nc.sync.dma_start(out=xraw[0][:, 0, :], in_=xf[:, 0, :])
+        nc.sync.dma_start(out=wbytes[0][:, 1, :], in_=wv[:, 0, 1, :])
         nc.sync.dma_start(out=xraw[0][:, 1, :], in_=xf[:, 1, :])
-        for r in range(1, 4):
-            nc.sync.dma_start(out=wbytes[0][:, r, :], in_=wv[:, 0, r, :])
-        load_w(1)
+        nc.sync.dma_start(out=wbytes[0][:, 2:4, :], in_=wv[:, 0, 2:4, :])
         load_x(1)
+        load_w(1)
         load_x(2)
         load_x(3)
-        nc.sync.dma_start(out=veraw[0][:, 1, :], in_=vef[:, 1, :])
         load_w(2)
-        load_ve(1)
+        load_ve(0)
         load_w(3)
+        load_ve(1)
+        load_w(4)
         load_ve(2)
         load_ve(3)
-        load_w(4)
         load_w(5)
 
         zeros = const.tile([P, 512], BF16, name="zeros")
@@ -103,8 +100,7 @@ def tile_causalselfattention_pa_kernel(tc, x, ve, qkv_w_bytes, qkv_w_scale, lamb
         nc.vector.tensor_tensor(out=frac[:], in0=turns_flat, in1=whole_i[:], op=ALU.subtract)
         negfrac = const.tile([P, 8 * NROT], F32, name="negfrac")
         nc.vector.scalar_tensor_tensor(out=negfrac[:], in0=frac[:], scalar=0.5, in1=frac[:], op0=ALU.is_gt, op1=ALU.subtract)
-        tab = const.tile([P, 2, 4, NROT], F32, name="tab")
-        nc.scalar.activation(out=tab[:].rearrange("p a j i -> p (a j i)"), in_=negfrac[:], func=ACT.Sin, scale=-2.0 * math.pi)
+        tab = const.tile([P, 4, 2, NROT], F32, name="tab")
         lam = const.tile([P, 2], F32, name="lam")
         nc.gpsimd.tensor_copy(out=lam[:], in_=lam_bf[:])
 
@@ -119,64 +115,71 @@ def tile_causalselfattention_pa_kernel(tc, x, ve, qkv_w_bytes, qkv_w_scale, lamb
         for k in range(NWARM):
             nc.tensor.matmul(out=warmbank[:], lhsT=zeros[:, 0:P], rhs=zeros[:], start=True, stop=True)
         warm = const.tile([P, 1], F32, name="warm")
-        nc.scalar.activation(out=warm[:], in_=eps[:], func=ACT.Abs_reciprocal_sqrt)
 
-        nc.scalar.activation(out=ve1[0][:], in_=veraw[0][:, 0, :], func=ACT.Copy, scale=lam[:, 1:2])
+        def sines():
+            for a in range(2):
+                nc.scalar.activation(out=tab[:, :, 1 - a, :], in_=negfrac[:].rearrange("p (a j i) -> p a j i", a=2, j=4)[:, a, :, :],
+                                     func=ACT.Sin, scale=-2.0 * math.pi)
 
-        for half in range(2):
-            sbank = psum.tile([P, 4, P], F32, name="tp", tag="tp", bufs=2)
-            for mm in range(4):
-                nc.tensor.transpose(sbank[:, mm, :], sc8[:, 4 * half + mm:4 * half + mm + 1].to_broadcast([P, P]), ident[:])
-            nc.vector.tensor_copy(out=scale_all[:].rearrange("p (n m) -> p n m", m=8)[:, :, 4 * half:4 * half + 4],
-                                  in_=sbank[:].rearrange("p m n -> p n m"))
+        def root_table():
+            nc.scalar.activation(out=warm[:], in_=eps[:], func=ACT.Abs_reciprocal_sqrt)
+
+        def bank_for_run():
+            st["runs"] = st.get("runs", 0) + 1
+            if st["runs"] <= HEADRUNS and st["runs"] % 4 in (1, 2):
+                return psum.tile([P, 2, 2, P], F32, name="acc", tag="acc", bufs=4)
+            if st["runs"] <= HEADRUNS and st["runs"] % 4 == 3:
+                return psum.tile([P, 2, 2, P], F32, name="vac", tag="vac", bufs=2)
+            return psum.tile([P, 2, 2, P], F32, name="tp", tag="tp", bufs=2)
 
         def transposes(key, words):
-            st["runs"] = st.get("runs", 0) + 1
-            if st["runs"] <= HEADRUNS and st["runs"] % 4 != 0:
-                tp = psum.tile([P, 2, 2, P], F32, name="acc", tag="acc", bufs=6)
-            else:
-                tp = psum.tile([P, 2, 2, P], F32, name="tp", tag="tp", bufs=2)
-            for g in range(2):
-                for u in range(2):
-                    nc.tensor.transpose(tp[:, g, u, :], words[:, 256 * g + u:256 * (g + 1):2], ident[:])
+            tp = bank_for_run()
+            for u in range(2):
+                for g in range(2):
+                    nc.tensor.transpose(tp[:, u, g, :], words[:, 256 * g + u:256 * (g + 1):2], ident[:])
             st[key] = tp
 
-        def x_transpose(i):
+        def x_turn(i):
             transposes(("xt", i), xraw[i // 2][:, i % 2, :].bitcast(F32))
-
-        def x_copy(i):
-            xg = stage.tile([P, 2, P, 2], F32, name="xg", tag="xg", bufs=5, align_bytes=64)
-            nc.scalar.copy(out=xg[:], in_=st["xt", i][:].rearrange("p g u r -> p g r u"))
+            xg = stage.tile([P, 256, 2], F32, name="xg", tag="xg", bufs=5, align_bytes=64)
+            nc.scalar.copy(out=xg[:], in_=st["xt", i][:].rearrange("p u g r -> p (g r) u"))
             st["xg", i] = xg
 
         def x_quant(i):
             nc.vector.quantize_mx(out=xc[i][:].bitcast(FP8X4), scales=xs[i][:],
-                                  in_=st["xg", i][:].rearrange("p g r u -> p (g r u)").bitcast(BF16))
+                                  in_=st["xg", i][:].rearrange("p r u -> p (r u)").bitcast(BF16))
 
-        def w_widen(rt):
-            wb = stage.tile([P, C], BF16, name="wb", tag="wb", bufs=6)
-            nc.vector.tensor_tensor(out=wb[:], in0=wbytes[rt // 4][:, rt % 4, :].bitcast(FP8), in1=scale_all[:], op=ALU.mult)
+        def w_cast(rt):
+            wb = stage.tile([P, C], BF16, name="wb", tag="wb", bufs=10)
+            src = wbytes[rt // 4][:, rt % 4, :].bitcast(FP8)
+            if rt in VCAST:
+                nc.vector.tensor_copy(out=wb[:], in_=src)
+            elif rt in SCAST:
+                nc.scalar.copy(out=wb[:], in_=src)
+            else:
+                nc.gpsimd.tensor_copy(out=wb[:], in_=src)
             st["wb", rt] = wb
 
         def w_transpose(rt):
             transposes(("wt", rt), st["wb", rt][:].bitcast(F32))
 
-        def w_copy(rt):
+        def w_mul(rt):
             c, r = divmod(rt, 4)
             if r == 0:
-                st["wg", c] = stage.tile([P, 2, 512, 2], F32, name="wg", tag="wg", bufs=2, align_bytes=64)
-            mover = nc.vector.tensor_copy if rt in VCOPY else nc.scalar.copy
-            mover(out=st["wg", c][:, :, r * P:(r + 1) * P, :], in_=st["wt", rt][:].rearrange("p g u r -> p g r u"))
+                st["wg", c] = stage.tile([P, 2, 4, 512], BF16, name="wg", tag="wg", bufs=2, align_bytes=64)
+            nc.vector.tensor_tensor(out=st["wg", c][:, :, r, :],
+                                    in0=st["wt", rt][:].bitcast(BF16).rearrange("p u g (r e) -> p (g r) u e", e=2),
+                                    in1=sck[:].unsqueeze(2).to_broadcast([P, 2, P, 4]), op=ALU.mult)
 
         def w_quant(c):
             nc.vector.quantize_mx(out=wc[c][:].bitcast(FP8X4), scales=ws[c][:],
-                                  in_=st["wg", c][:].rearrange("p g r u -> p (g r u)").bitcast(BF16))
+                                  in_=st["wg", c][:].rearrange("p g r m -> p (g r m)"))
 
-        def project(key, tt, sec, tag, bufs):
+        def matmuls(c, m, tag, bufs):
             banks = []
             for half in range(2):
                 acc = psum.tile([P, 512], F32, name=tag, tag=tag, bufs=bufs)
-                c = 2 * sec + half
+                tt = 2 * m + half
                 for g in range(2):
                     nc.tensor.matmul_mx(out=acc[:],
                                         lhsT=xc[tt][:, g * P:(g + 1) * P].bitcast(FP8X4),
@@ -185,100 +188,114 @@ def tile_causalselfattention_pa_kernel(tc, x, ve, qkv_w_bytes, qkv_w_scale, lamb
                                         rhs_scale=ws[c][:, g * 512:(g + 1) * 512],
                                         start=(g == 0), stop=(g == 1))
                 banks.append(acc)
-            st[key] = banks
+            st["acc", c, m] = banks
 
-        def matmuls(u):
-            project(("acc", u), u % 8, u // 8, "acc", 6)
+        def unit(s):
+            return s // 4, s % 4
 
-        def head_cols(u, h):
-            return st["acc", u][h // 4][:, (h % 4) * D:(h % 4 + 1) * D]
+        def mm(s):
+            if s < 16:
+                matmuls(unit(s)[0], unit(s)[1], "acc", 4)
 
-        def squares(u):
-            ss = stage.tile([P, HEADS], F32, name="ss", tag="ss", bufs=4)
-            o = stage.tile([P, HEADS * D], F32, name="o", tag="o", bufs=6)
-            st["o", u] = o
-            for h in range(HEADS):
-                nc.scalar.activation(out=o[:, h * D:(h + 1) * D], in_=head_cols(u, h), func=ACT.Square, accum_out=ss[:, h:h + 1])
-            st["ss", u] = ss
-
-        def root(u):
-            rinv = stage.tile([P, HEADS], F32, name="rinv", tag="rinv", bufs=4)
-            nc.scalar.activation(out=rinv[:], in_=st["ss", u][:], func=ACT.Abs_reciprocal_sqrt, bias=eps[:, 0:1], scale=1.0 / D)
-            st["rinv", u] = rinv
-
-        def recip(u):
-            return
-
-        def normalise(u):
-            o = st["o", u]
-            if u in VNORM:
-                for b in range(2):
-                    nc.vector.tensor_tensor(out=o[:, b * 512:(b + 1) * 512].rearrange("p (h d) -> p h d", d=D),
-                                            in0=st["acc", u][b][:].rearrange("p (h d) -> p h d", d=D),
-                                            in1=st["rinv", u][:, 4 * b:4 * b + 4].unsqueeze(2).to_broadcast([P, 4, D]), op=ALU.mult)
+        def squares(s):
+            if not 0 <= s < 16:
                 return
-            for h in range(HEADS):
-                nc.scalar.activation(out=o[:, h * D:(h + 1) * D], in_=head_cols(u, h), func=ACT.Copy,
-                                     scale=st["rinv", u][:, h:h + 1])
+            banks = st["acc", unit(s)[0], unit(s)[1]]
+            ss = stage.tile([P, 2, 4], F32, name="ss", tag="ss", bufs=4)
+            o = stage.tile([P, 2, 4, D], F32, name="o", tag="o", bufs=6)
+            for b in range(2):
+                for h in range(4):
+                    nc.scalar.activation(out=o[:, b, h, :], in_=banks[b][:, h * D:(h + 1) * D], func=ACT.Square, accum_out=ss[:, b, h:h + 1])
+            st["ss", s] = ss
+            st["o", s] = o
 
-        def rope_mul(u, h0=0, nh=HEADS):
-            j = u % 4
-            rot = st["o", u][:, h0 * D:(h0 + nh) * D].rearrange("p (m d) -> p m d", d=64)[:, :, 0:NROT]
-            ra = stage.tile([P, 2 * nh, NROT], F32, name="ra", tag="ra", bufs=2)
-            rb = stage.tile([P, 2 * nh, NROT], F32, name="rb", tag="rb", bufs=2)
-            nc.vector.tensor_tensor(out=ra[:], in0=rot, in1=tab[:, 1, j, :].unsqueeze(1).to_broadcast([P, 2 * nh, NROT]), op=ALU.mult)
-            nc.vector.tensor_tensor(out=rb[:], in0=rot, in1=tab[:, 0, j, :].unsqueeze(1).to_broadcast([P, 2 * nh, NROT]), op=ALU.mult)
-            st["ra", u, h0] = ra
-            st["rb", u, h0] = rb
+        def root(s):
+            if not 0 <= s < 16:
+                return
+            rinv = stage.tile([P, 2, 2, 4], F32, name="rinv", tag="rinv", bufs=4)
+            nc.scalar.activation(out=rinv[:], in_=st["ss", s][:].unsqueeze(2).to_broadcast([P, 2, 2, 4]), func=ACT.Abs_reciprocal_sqrt,
+                                 bias=eps[:, 0:1], scale=1.0 / D)
+            st["rinv", s] = rinv
 
-        def rope_add(u, h0=0, nh=HEADS):
-            cols = slice(h0 * D, (h0 + nh) * D)
-            o4 = st["o", u][:, cols].rearrange("p (h w d) -> p h w d", w=2, d=64)
-            a4 = st["ra", u, h0][:].rearrange("p (h w) i -> p h w i", w=2)
-            b4 = st["rb", u, h0][:].rearrange("p (h w) i -> p h w i", w=2)
-            nc.vector.tensor_tensor(out=o4[:, :, 0, 0:NROT], in0=a4[:, :, 0, :], in1=b4[:, :, 1, :], op=ALU.add)
-            nc.vector.tensor_tensor(out=o4[:, :, 1, 0:NROT], in0=a4[:, :, 1, :], in1=b4[:, :, 0, :], op=ALU.subtract)
-            tt = u % 8
-            nc.sync.dma_start(out=outs[u // 8][tt * P:(tt + 1) * P, cols], in_=st["o", u][:, cols])
+        def tables(s):
+            if not 0 <= s < 16:
+                return
+            rtab = stage.tile([P, 16, NROT], F32, name="rtab", tag="rtab", bufs=3)
+            j = (2 * unit(s)[1]) % 4
+            nc.gpsimd.tensor_tensor(out=rtab[:].rearrange("p (a h) i -> p a h i", h=4),
+                                    in0=tab[:, j:j + 2, :, :].rearrange("p b c i -> p (b c) i").unsqueeze(2).to_broadcast([P, 4, 4, NROT]),
+                                    in1=st["rinv", s][:].rearrange("p b c h -> p (b c) h").unsqueeze(3).to_broadcast([P, 4, 4, NROT]), op=ALU.mult)
+            st["rtab", s] = rtab
+
+        def unrotated(s):
+            if not 0 <= s < 16:
+                return
+            banks = st["acc", unit(s)[0], unit(s)[1]]
+            for b in range(2):
+                for h in range(4):
+                    nc.scalar.activation(out=st["o", s][:, b, h, :].rearrange("p (w d) -> p w d", w=2)[:, :, NROT:64],
+                                         in_=banks[b][:, h * D:(h + 1) * D].rearrange("p (w d) -> p w d", w=2)[:, :, NROT:64],
+                                         func=ACT.Copy, scale=st["rinv", s][:, b, 0, h:h + 1])
+
+        def products(s):
+            if not 0 <= s < 16:
+                return
+            banks = st["acc", unit(s)[0], unit(s)[1]]
+            rab = stage.tile([P, 2, 2, 8, NROT], F32, name="rab", tag="rab", bufs=3)
+            for b in range(2):
+                nc.vector.tensor_tensor(out=rab[:, b, :, :, :],
+                                        in0=banks[b][:].rearrange("p (m d) -> p m d", d=64)[:, :, 0:NROT].unsqueeze(1).to_broadcast([P, 2, 8, NROT]),
+                                        in1=st["rtab", s][:, 8 * b:8 * b + 8, :].unsqueeze(2).to_broadcast([P, 8, 2, NROT]), op=ALU.mult)
+            st["rab", s] = rab
+
+        def adds(s):
+            if not 0 <= s < 16:
+                return
+            c, m = unit(s)
+            r6 = st["rab", s][:].rearrange("p b c (h w) i -> p b c h w i", w=2)
+            o6 = st["o", s][:].rearrange("p b h (w d) -> p (b h) w d", w=2)
+            eng = nc.vector if s in VADD else nc.gpsimd
+            eng.tensor_tensor(out=o6[:, :, 0, 0:NROT], in0=r6[:, :, 0, :, 0, :], in1=r6[:, :, 1, :, 1, :], op=ALU.add)
+            eng.tensor_tensor(out=o6[:, :, 1, 0:NROT], in0=r6[:, :, 0, :, 1, :], in1=r6[:, :, 1, :, 0, :], op=ALU.subtract)
+            nc.sync.dma_start(out=outs[c // 2][:, 2 * m:2 * m + 2, (c % 2) * 512:(c % 2 + 1) * 512],
+                              in_=st["o", s][:].rearrange("p b h d -> p b (h d)"))
 
         def ve_scale(tt):
             nc.scalar.activation(out=ve1[tt][:], in_=veraw[tt // 2][:, tt % 2, :], func=ACT.Copy, scale=lam[:, 1:2])
 
-        def value_matmuls(tt):
-            project(("accv", tt), tt, 2, "tp", 2)
-
-        def value_blend(tt, half):
+        def blend(v, half):
+            c, m = 4 + v // 4, v % 4
             if half == 0:
-                st["ov", tt] = stage.tile([P, HEADS * D], F32, name="ov", tag="ov", bufs=3)
-            cols = slice(half * 512, (half + 1) * 512)
-            nc.vector.scalar_tensor_tensor(out=st["ov", tt][:, cols], in0=st["accv", tt][half][:], scalar=lam[:, 0:1],
-                                           in1=ve1[tt][:, cols], op0=ALU.mult, op1=ALU.add)
-            nc.sync.dma_start(out=outs[2][tt * P:(tt + 1) * P, cols], in_=st["ov", tt][:, cols])
+                st["ov", v] = stage.tile([P, 2, 512], F32, name="ov", tag="ov", bufs=3)
+            cols = slice((c % 2) * 512, (c % 2 + 1) * 512)
+            nc.vector.scalar_tensor_tensor(out=st["ov", v][:, half, :], in0=st["acc", c, m][half][:], scalar=lam[:, 0:1],
+                                           in1=ve1[2 * m + half][:, cols], op0=ALU.mult, op1=ALU.add)
+            nc.sync.dma_start(out=outs[2][:, 2 * m + half, cols], in_=st["ov", v][:, half, :])
 
-        q = {"w": 0, "c": 0, "z": 0, "xq": 0, "ve": 1}
+        q = {"cast": 0, "turn": 0, "mul": 0, "z": 0, "ve": 0}
 
-        def widen(n):
+        def cast(n):
             for k in range(n):
-                if q["w"] < 24:
-                    w_widen(q["w"])
-                    w_transpose(q["w"])
-                    q["w"] += 1
+                if q["cast"] < 24:
+                    w_cast(q["cast"])
+                    q["cast"] += 1
 
-        def copy(n):
+        def turn(n):
             for k in range(n):
-                if q["c"] < q["w"]:
-                    w_copy(q["c"])
-                    q["c"] += 1
+                if q["turn"] < q["cast"]:
+                    w_transpose(q["turn"])
+                    q["turn"] += 1
+
+        def mul(n):
+            for k in range(n):
+                if q["mul"] < q["turn"]:
+                    w_mul(q["mul"])
+                    q["mul"] += 1
 
         def quant():
-            if q["z"] < 6 and q["c"] >= 4 * q["z"] + 4:
+            if q["z"] < 6 and q["mul"] >= 4 * q["z"] + 4:
                 w_quant(q["z"])
                 q["z"] += 1
-
-        def xquant(upto):
-            while q["xq"] <= upto:
-                x_quant(q["xq"])
-                q["xq"] += 1
 
         def vescale(n):
             for k in range(n):
@@ -286,65 +303,67 @@ def tile_causalselfattention_pa_kernel(tc, x, ve, qkv_w_bytes, qkv_w_scale, lamb
                     ve_scale(q["ve"])
                     q["ve"] += 1
 
-        def x_turn(i):
-            x_transpose(i)
-            x_copy(i)
-
-        for i in range(8):
-            x_turn(i)
-            widen(1)
-            copy(1)
-            xquant(i - XLAG)
-            if i == 6:
-                quant()
-            if i >= 6:
-                vescale(1)
-        widen(2)
-        xquant(7)
+        sines()
+        cast(1)
+        turn(1)
+        x_turn(0)
+        cast(3)
+        mul(1)
+        x_quant(0)
+        turn(1)
+        x_turn(1)
+        mul(1)
+        x_quant(1)
+        turn(2)
+        mul(1)
+        x_turn(2)
+        cast(3)
+        x_turn(3)
+        mul(1)
+        x_quant(2)
         quant()
-        copy(1)
-        matmuls(0)
-        vescale(1)
-        copy(1)
-        matmuls(1)
-        vescale(1)
-        squares(0)
-        widen(1)
-        copy(1)
-        root(0)
-        widen(NBRIDGE - 3)
-        recip(0)
+        x_turn(4)
+        x_turn(5)
+        root_table()
+        turn(1)
+        mul(1)
+        x_quant(3)
+        mm(0)
+        turn(1)
+        mm(1)
+        mul(1)
+        x_turn(6)
+        x_turn(7)
+        cast(5)
+        turn(1)
 
-        for t in range(17):
-            if t + 2 <= 15:
-                matmuls(t + 2)
-            if t + 1 <= 15:
-                squares(t + 1)
-            copy(1)
-            if t + 1 <= 15:
-                root(t + 1)
-            if 1 <= t <= 15:
-                rope_mul(t - 1)
-            if t == 16:
-                rope_mul(15, 0, 4)
-                rope_mul(15, 4, 4)
-                rope_add(15, 0, 4)
-                rope_add(15, 4, 4)
-            widen(1)
-            if EV0 <= t <= EV0 + 7:
-                value_blend(t - EV0, 0)
-            if t <= 15:
-                normalise(t)
-            if 1 <= t <= 15:
-                rope_add(t - 1)
-            copy(1)
-            widen(1)
+        for s in range(-2, 17):
+            products(s)
+            tables(s + 1)
+            if s >= 0:
+                mm(s + 2)
+            squares(s + 2)
             quant()
-            if EV0 <= t <= EV0 + 7:
-                value_blend(t - EV0, 1)
-            if t + 1 <= 15:
-                recip(t + 1)
-            if EV0 - 1 <= t <= EV0 + 6:
-                value_matmuls(t - EV0 + 1)
-            if t <= 3:
-                vescale(1)
+            cast(1)
+            root(s + 2)
+            unrotated(s + 2)
+            turn(1)
+            mul(1)
+            if s == -2:
+                x_quant(4)
+                x_quant(5)
+            if s == -1:
+                x_quant(6)
+                x_quant(7)
+            adds(s)
+            if s < 6:
+                cast(1)
+                turn(1)
+                mul(1)
+            if V0 <= s < V0 + 8:
+                blend(s - V0, 0)
+                blend(s - V0, 1)
+            if V0 - 1 <= s < V0 + 7:
+                v = s - V0 + 1
+                matmuls(4 + v // 4, v % 4, "vac", 2)
+            vescale(1)

@@ -25,10 +25,11 @@ EPS = 2.0 ** -23
 RATIO = (1.0 / 1024.0) ** (1.0 / 31.0)
 HEADRUNS = 12
 NWARM = 4
-VADD = (9, 11, 13, 15)
+VADD = (15,)
 V0 = 8
+ACC, TP, VB = 5, 2, 1
 VCAST = (0, 1)
-SCAST = (4, 6, 8, 11, 14, 17, 20, 23)
+SCAST = (2, 3) + tuple(k for k in range(9, 24) if k % 3)
 
 
 def tile_causalselfattention_pa_kernel(tc, x, ve, qkv_w_bytes, qkv_w_scale, lambdas, out_0, out_1, out_2):
@@ -62,18 +63,17 @@ def tile_causalselfattention_pa_kernel(tc, x, ve, qkv_w_bytes, qkv_w_scale, lamb
         def load_ve(i):
             nc.sync.dma_start(out=veraw[i][:], in_=vef[:, 2 * i:2 * i + 2, :])
 
-        nc.sync.dma_start(out=wbytes[0][:, 0, :], in_=wv[:, 0, 0, :])
-        nc.sync.dma_start(out=xraw[0][:, 0, :], in_=xf[:, 0, :])
-        nc.sync.dma_start(out=wbytes[0][:, 1, :], in_=wv[:, 0, 1, :])
-        nc.sync.dma_start(out=xraw[0][:, 1, :], in_=xf[:, 1, :])
-        nc.sync.dma_start(out=wbytes[0][:, 2:4, :], in_=wv[:, 0, 2:4, :])
+        for r in range(4):
+            nc.sync.dma_start(out=wbytes[0][:, r, :], in_=wv[:, 0, r, :])
+        for i in range(2):
+            nc.sync.dma_start(out=xraw[0][:, i, :], in_=xf[:, i, :])
         load_x(1)
         load_w(1)
         load_x(2)
         load_x(3)
         load_w(2)
-        load_ve(0)
         load_w(3)
+        load_ve(0)
         load_ve(1)
         load_w(4)
         load_ve(2)
@@ -92,26 +92,35 @@ def tile_causalselfattention_pa_kernel(tc, x, ve, qkv_w_bytes, qkv_w_scale, lamb
         nc.vector.tensor_scalar(out=turns[:, 0, :, 0], in0=tpos[:], scalar1=1.0 / (2.0 * math.pi), scalar2=None, op0=ALU.mult)
         for n in (1, 2, 4, 8, 16):
             nc.vector.tensor_scalar(out=turns[:, 0, :, n:2 * n], in0=turns[:, 0, :, 0:n], scalar1=RATIO ** n, scalar2=None, op0=ALU.mult)
-        nc.vector.tensor_scalar(out=turns[:, 1, :, :], in0=turns[:, 0, :, :], scalar1=0.25, scalar2=None, op0=ALU.add)
         turns_flat = turns[:].rearrange("p a j i -> p (a j i)")
         whole_i = const.tile([P, 8 * NROT], I32, name="whole_i")
-        nc.vector.tensor_copy(out=whole_i[:], in_=turns_flat)
         frac = const.tile([P, 8 * NROT], F32, name="frac")
-        nc.vector.tensor_tensor(out=frac[:], in0=turns_flat, in1=whole_i[:], op=ALU.subtract)
         negfrac = const.tile([P, 8 * NROT], F32, name="negfrac")
-        nc.vector.scalar_tensor_tensor(out=negfrac[:], in0=frac[:], scalar=0.5, in1=frac[:], op0=ALU.is_gt, op1=ALU.subtract)
+
+        def quarter_turn():
+            nc.vector.tensor_scalar(out=turns[:, 1, :, :], in0=turns[:, 0, :, :], scalar1=0.25, scalar2=None, op0=ALU.add)
+
+        def whole_turns():
+            nc.vector.tensor_copy(out=whole_i[:], in_=turns_flat)
+
+        def fractions():
+            nc.vector.tensor_tensor(out=frac[:], in0=turns_flat, in1=whole_i[:], op=ALU.subtract)
+
+        def half_turns():
+            nc.vector.scalar_tensor_tensor(out=negfrac[:], in0=frac[:], scalar=0.5, in1=frac[:], op0=ALU.is_gt, op1=ALU.subtract)
+
         tab = const.tile([P, 4, 2, NROT], F32, name="tab")
         lam = const.tile([P, 2], F32, name="lam")
         nc.gpsimd.tensor_copy(out=lam[:], in_=lam_bf[:])
 
-        xc = [keep.tile([P, 256], U32, name="xc%d" % i, align_bytes=64) for i in range(8)]
-        xs = [keep.tile([P, 256], U8, name="xs%d" % i, align_bytes=64) for i in range(8)]
+        xc = [keep.tile([P, 512], U32, name="xc%d" % m, align_bytes=64) for m in range(4)]
+        xs = [keep.tile([P, 512], U8, name="xs%d" % m, align_bytes=64) for m in range(4)]
         wc = [keep.tile([P, 1024], U32, name="wc%d" % c, align_bytes=64) for c in range(6)]
         ws = [keep.tile([P, 1024], U8, name="ws%d" % c, align_bytes=64) for c in range(6)]
         ve1 = [keep.tile([P, C], F32, name="ve1_%d" % i) for i in range(8)]
         st = {}
 
-        warmbank = psum.tile([P, 512], F32, name="tp", tag="tp", bufs=2)
+        warmbank = psum.tile([P, 512], F32, name="tp", tag="tp", bufs=TP)
         for k in range(NWARM):
             nc.tensor.matmul(out=warmbank[:], lhsT=zeros[:, 0:P], rhs=zeros[:], start=True, stop=True)
         warm = const.tile([P, 1], F32, name="warm")
@@ -125,12 +134,12 @@ def tile_causalselfattention_pa_kernel(tc, x, ve, qkv_w_bytes, qkv_w_scale, lamb
             nc.scalar.activation(out=warm[:], in_=eps[:], func=ACT.Abs_reciprocal_sqrt)
 
         def bank_for_run():
-            st["runs"] = st.get("runs", 0) + 1
-            if st["runs"] <= HEADRUNS and st["runs"] % 4 in (1, 2):
-                return psum.tile([P, 2, 2, P], F32, name="acc", tag="acc", bufs=4)
-            if st["runs"] <= HEADRUNS and st["runs"] % 4 == 3:
-                return psum.tile([P, 2, 2, P], F32, name="vac", tag="vac", bufs=2)
-            return psum.tile([P, 2, 2, P], F32, name="tp", tag="tp", bufs=2)
+            r = st["runs"] = st.get("runs", -1) + 1
+            if r < HEADRUNS and r % 8 < ACC:
+                return psum.tile([P, 2, 2, P], F32, name="acc", tag="acc", bufs=ACC)
+            if r < HEADRUNS and r % 8 < ACC + VB:
+                return psum.tile([P, 2, 2, P], F32, name="vac", tag="vac", bufs=VB)
+            return psum.tile([P, 2, 2, P], F32, name="tp", tag="tp", bufs=TP)
 
         def transposes(key, words):
             tp = bank_for_run()
@@ -141,16 +150,16 @@ def tile_causalselfattention_pa_kernel(tc, x, ve, qkv_w_bytes, qkv_w_scale, lamb
 
         def x_turn(i):
             transposes(("xt", i), xraw[i // 2][:, i % 2, :].bitcast(F32))
-            xg = stage.tile([P, 256, 2], F32, name="xg", tag="xg", bufs=5, align_bytes=64)
-            nc.scalar.copy(out=xg[:], in_=st["xt", i][:].rearrange("p u g r -> p (g r) u"))
-            st["xg", i] = xg
+            if i % 2 == 0:
+                st["xg", i // 2] = stage.tile([P, 2, 256, 2], F32, name="xg", tag="xg", bufs=3, align_bytes=64)
+            nc.scalar.copy(out=st["xg", i // 2][:, i % 2, :, :], in_=st["xt", i][:].rearrange("p u g r -> p (g r) u"))
 
-        def x_quant(i):
-            nc.vector.quantize_mx(out=xc[i][:].bitcast(FP8X4), scales=xs[i][:],
-                                  in_=st["xg", i][:].rearrange("p r u -> p (r u)").bitcast(BF16))
+        def x_quant(m):
+            nc.vector.quantize_mx(out=xc[m][:].bitcast(FP8X4), scales=xs[m][:],
+                                  in_=st["xg", m][:].rearrange("p i r u -> p (i r u)").bitcast(BF16))
 
         def w_cast(rt):
-            wb = stage.tile([P, C], BF16, name="wb", tag="wb", bufs=10)
+            wb = stage.tile([P, C], BF16, name="wb", tag="wb", bufs=8)
             src = wbytes[rt // 4][:, rt % 4, :].bitcast(FP8)
             if rt in VCAST:
                 nc.vector.tensor_copy(out=wb[:], in_=src)
@@ -175,32 +184,34 @@ def tile_causalselfattention_pa_kernel(tc, x, ve, qkv_w_bytes, qkv_w_scale, lamb
             nc.vector.quantize_mx(out=wc[c][:].bitcast(FP8X4), scales=ws[c][:],
                                   in_=st["wg", c][:].rearrange("p g r m -> p (g r m)"))
 
-        def matmuls(c, m, tag, bufs):
-            banks = []
-            for half in range(2):
-                acc = psum.tile([P, 512], F32, name=tag, tag=tag, bufs=bufs)
-                tt = 2 * m + half
-                for g in range(2):
-                    nc.tensor.matmul_mx(out=acc[:],
-                                        lhsT=xc[tt][:, g * P:(g + 1) * P].bitcast(FP8X4),
-                                        lhsT_scale=xs[tt][:, g * P:(g + 1) * P],
-                                        rhs=wc[c][:, g * 512:(g + 1) * 512].bitcast(FP8X4),
-                                        rhs_scale=ws[c][:, g * 512:(g + 1) * 512],
-                                        start=(g == 0), stop=(g == 1))
-                banks.append(acc)
-            st["acc", c, m] = banks
+        def project(c, tt, tag, bufs):
+            acc = psum.tile([P, 512], F32, name=tag, tag=tag, bufs=bufs)
+            for g in range(2):
+                rows = slice((2 * (tt % 2) + g) * P, (2 * (tt % 2) + g + 1) * P)
+                nc.tensor.matmul_mx(out=acc[:],
+                                    lhsT=xc[tt // 2][:, rows].bitcast(FP8X4),
+                                    lhsT_scale=xs[tt // 2][:, rows],
+                                    rhs=wc[c][:, g * 512:(g + 1) * 512].bitcast(FP8X4),
+                                    rhs_scale=ws[c][:, g * 512:(g + 1) * 512],
+                                    start=(g == 0), stop=(g == 1))
+            return acc
 
         def unit(s):
             return s // 4, s % 4
 
-        def mm(s):
+        def mm(s, half):
+            c, m = unit(s)
             if s < 16:
-                matmuls(unit(s)[0], unit(s)[1], "acc", 4)
+                st["acc", c, m, half] = project(c, 2 * m + half, "acc", ACC)
+
+        def banks_of(s):
+            c, m = unit(s)
+            return [st["acc", c, m, half] for half in range(2)]
 
         def squares(s):
             if not 0 <= s < 16:
                 return
-            banks = st["acc", unit(s)[0], unit(s)[1]]
+            banks = banks_of(s)
             ss = stage.tile([P, 2, 4], F32, name="ss", tag="ss", bufs=4)
             o = stage.tile([P, 2, 4, D], F32, name="o", tag="o", bufs=6)
             for b in range(2):
@@ -230,7 +241,7 @@ def tile_causalselfattention_pa_kernel(tc, x, ve, qkv_w_bytes, qkv_w_scale, lamb
         def unrotated(s):
             if not 0 <= s < 16:
                 return
-            banks = st["acc", unit(s)[0], unit(s)[1]]
+            banks = banks_of(s)
             for b in range(2):
                 for h in range(4):
                     nc.scalar.activation(out=st["o", s][:, b, h, :].rearrange("p (w d) -> p w d", w=2)[:, :, NROT:64],
@@ -240,7 +251,7 @@ def tile_causalselfattention_pa_kernel(tc, x, ve, qkv_w_bytes, qkv_w_scale, lamb
         def products(s):
             if not 0 <= s < 16:
                 return
-            banks = st["acc", unit(s)[0], unit(s)[1]]
+            banks = banks_of(s)
             rab = stage.tile([P, 2, 2, 8, NROT], F32, name="rab", tag="rab", bufs=3)
             for b in range(2):
                 nc.vector.tensor_tensor(out=rab[:, b, :, :, :],
@@ -263,16 +274,18 @@ def tile_causalselfattention_pa_kernel(tc, x, ve, qkv_w_bytes, qkv_w_scale, lamb
         def ve_scale(tt):
             nc.scalar.activation(out=ve1[tt][:], in_=veraw[tt // 2][:, tt % 2, :], func=ACT.Copy, scale=lam[:, 1:2])
 
-        def blend(v, half):
-            c, m = 4 + v // 4, v % 4
-            if half == 0:
-                st["ov", v] = stage.tile([P, 2, 512], F32, name="ov", tag="ov", bufs=3)
-            cols = slice((c % 2) * 512, (c % 2 + 1) * 512)
-            nc.vector.scalar_tensor_tensor(out=st["ov", v][:, half, :], in0=st["acc", c, m][half][:], scalar=lam[:, 0:1],
-                                           in1=ve1[2 * m + half][:, cols], op0=ALU.mult, op1=ALU.add)
-            nc.sync.dma_start(out=outs[2][:, 2 * m + half, cols], in_=st["ov", v][:, half, :])
+        def vmm(n):
+            spare = q["turn"] == 24 and n % 3 != 0
+            st["v", n] = project(4 + n // 8, n % 8, "tp" if spare else "vac", TP if spare else VB)
 
-        q = {"cast": 0, "turn": 0, "mul": 0, "z": 0, "ve": 0}
+        def blend(n):
+            ov = stage.tile([P, 512], F32, name="ov", tag="ov", bufs=6)
+            cols = slice(n // 8 * 512, (n // 8 + 1) * 512)
+            nc.vector.scalar_tensor_tensor(out=ov[:], in0=st["v", n][:], scalar=lam[:, 0:1],
+                                           in1=ve1[n % 8][:, cols], op0=ALU.mult, op1=ALU.add)
+            nc.sync.dma_start(out=outs[2][:, n % 8, cols], in_=ov[:])
+
+        q = {"cast": 0, "turn": 0, "mul": 0, "z": 0, "ve": 0, "v": 0, "vm": 0}
 
         def cast(n):
             for k in range(n):
@@ -297,73 +310,83 @@ def tile_causalselfattention_pa_kernel(tc, x, ve, qkv_w_bytes, qkv_w_scale, lamb
                 w_quant(q["z"])
                 q["z"] += 1
 
+        def vahead():
+            while q["vm"] < min(16, 8 if q["z"] < 6 else 16, q["v"] + (3 if q["turn"] == 24 else 1)):
+                vmm(q["vm"])
+                q["vm"] += 1
+
+        def vblend():
+            if q["v"] < q["vm"]:
+                blend(q["v"])
+                q["v"] += 1
+                vahead()
+
         def vescale(n):
             for k in range(n):
                 if q["ve"] < 8:
                     ve_scale(q["ve"])
                     q["ve"] += 1
 
-        sines()
+        quarter_turn()
+        cast(1)
+        whole_turns()
+        cast(1)
+        fractions()
+        turn(1)
         cast(1)
         turn(1)
+        cast(1)
         x_turn(0)
-        cast(3)
-        mul(1)
-        x_quant(0)
-        turn(1)
         x_turn(1)
+        turn(1)
         mul(1)
-        x_quant(1)
-        turn(2)
+        half_turns()
+        turn(1)
         mul(1)
         x_turn(2)
-        cast(3)
         x_turn(3)
+        sines()
         mul(1)
-        x_quant(2)
+        x_quant(0)
+        mul(1)
+        x_quant(1)
         quant()
+        cast(6)
         x_turn(4)
         x_turn(5)
         root_table()
-        turn(1)
+        turn(2)
         mul(1)
-        x_quant(3)
-        mm(0)
-        turn(1)
-        mm(1)
-        mul(1)
+        x_quant(2)
         x_turn(6)
         x_turn(7)
-        cast(5)
-        turn(1)
+        mm(0, 0)
+        mul(1)
+        turn(2)
+        x_quant(3)
 
-        for s in range(-2, 17):
+        for s in range(-2, 18):
             products(s)
+            mm(s + 2, 1)
+            mm(s + 3, 0)
             tables(s + 1)
-            if s >= 0:
-                mm(s + 2)
+            adds(s - 1)
             squares(s + 2)
-            quant()
-            cast(1)
             root(s + 2)
-            unrotated(s + 2)
-            turn(1)
+            quant()
             mul(1)
-            if s == -2:
-                x_quant(4)
-                x_quant(5)
-            if s == -1:
-                x_quant(6)
-                x_quant(7)
-            adds(s)
-            if s < 6:
-                cast(1)
-                turn(1)
+            turn(1)
+            cast(1)
+            if s >= V0:
+                vblend()
+            unrotated(s + 2)
+            if s % 2 == 0:
                 mul(1)
-            if V0 <= s < V0 + 8:
-                blend(s - V0, 0)
-                blend(s - V0, 1)
-            if V0 - 1 <= s < V0 + 7:
-                v = s - V0 + 1
-                matmuls(4 + v // 4, v % 4, "vac", 2)
-            vescale(1)
+                turn(1)
+                cast(1)
+            if s >= V0:
+                vblend()
+            if s >= V0 - 1:
+                vahead()
+            if s >= 3:
+                vescale(1)

@@ -29,7 +29,7 @@ VADD = (15,)
 V0 = 8
 ACC, TP, VB = 5, 2, 1
 VCAST = (0, 1)
-SCAST = (2, 3) + tuple(k for k in range(9, 24) if k % 3)
+SCAST = (2, 3) + tuple(range(10, 24))
 
 
 def tile_causalselfattention_pa_kernel(tc, x, ve, qkv_w_bytes, qkv_w_scale, lambdas, out_0, out_1, out_2):
@@ -71,10 +71,10 @@ def tile_causalselfattention_pa_kernel(tc, x, ve, qkv_w_bytes, qkv_w_scale, lamb
         load_w(1)
         load_x(2)
         load_x(3)
-        load_w(2)
-        load_w(3)
         load_ve(0)
+        load_w(2)
         load_ve(1)
+        load_w(3)
         load_w(4)
         load_ve(2)
         load_ve(3)
@@ -262,12 +262,16 @@ def tile_causalselfattention_pa_kernel(tc, x, ve, qkv_w_bytes, qkv_w_scale, lamb
         def adds(s):
             if not 0 <= s < 16:
                 return
-            c, m = unit(s)
             r6 = st["rab", s][:].rearrange("p b c (h w) i -> p b c h w i", w=2)
             o6 = st["o", s][:].rearrange("p b h (w d) -> p (b h) w d", w=2)
             eng = nc.vector if s in VADD else nc.gpsimd
             eng.tensor_tensor(out=o6[:, :, 0, 0:NROT], in0=r6[:, :, 0, :, 0, :], in1=r6[:, :, 1, :, 1, :], op=ALU.add)
             eng.tensor_tensor(out=o6[:, :, 1, 0:NROT], in0=r6[:, :, 0, :, 1, :], in1=r6[:, :, 1, :, 0, :], op=ALU.subtract)
+
+        def store(s):
+            if not 0 <= s < 16:
+                return
+            c, m = unit(s)
             nc.sync.dma_start(out=outs[c // 2][:, 2 * m:2 * m + 2, (c % 2) * 512:(c % 2 + 1) * 512],
                               in_=st["o", s][:].rearrange("p b h d -> p b (h d)"))
 
@@ -354,12 +358,13 @@ def tile_causalselfattention_pa_kernel(tc, x, ve, qkv_w_bytes, qkv_w_scale, lamb
         cast(6)
         x_turn(4)
         x_turn(5)
-        root_table()
         turn(2)
         mul(1)
         x_quant(2)
+        vescale(1)
         x_turn(6)
         x_turn(7)
+        root_table()
         mm(0, 0)
         mul(1)
         turn(2)
@@ -388,5 +393,6 @@ def tile_causalselfattention_pa_kernel(tc, x, ve, qkv_w_bytes, qkv_w_scale, lamb
                 vblend()
             if s >= V0 - 1:
                 vahead()
+            store(s - 1)
             if s >= 3:
                 vescale(1)

@@ -25,11 +25,12 @@ EPS = 2.0 ** -23
 RATIO = (1.0 / 1024.0) ** (1.0 / 31.0)
 HEADRUNS = 12
 NWARM = 4
-VADD = (15,)
+VADD = (13, 14, 15)
 V0 = 8
 ACC, TP, VB = 5, 2, 1
+SROT = ()
 VCAST = (0, 1)
-SCAST = (2, 3) + tuple(range(10, 24))
+SCAST = (2, 3, 5, 7) + tuple(range(9, 24))
 
 
 def tile_causalselfattention_pa_kernel(tc, x, ve, qkv_w_bytes, qkv_w_scale, lambdas, out_0, out_1, out_2):
@@ -159,7 +160,7 @@ def tile_causalselfattention_pa_kernel(tc, x, ve, qkv_w_bytes, qkv_w_scale, lamb
                                   in_=st["xg", m][:].rearrange("p i r u -> p (i r u)").bitcast(BF16))
 
         def w_cast(rt):
-            wb = stage.tile([P, C], BF16, name="wb", tag="wb", bufs=8)
+            wb = stage.tile([P, C], BF16, name="wb", tag="wb", bufs=10)
             src = wbytes[rt // 4][:, rt % 4, :].bitcast(FP8)
             if rt in VCAST:
                 nc.vector.tensor_copy(out=wb[:], in_=src)
@@ -213,30 +214,19 @@ def tile_causalselfattention_pa_kernel(tc, x, ve, qkv_w_bytes, qkv_w_scale, lamb
                 return
             banks = banks_of(s)
             ss = stage.tile([P, 2, 4], F32, name="ss", tag="ss", bufs=4)
-            o = stage.tile([P, 2, 4, D], F32, name="o", tag="o", bufs=6)
+            sq = stage.tile([P, 2, 4, D], BF16, name="sq", tag="sq", bufs=2)
             for b in range(2):
                 for h in range(4):
-                    nc.scalar.activation(out=o[:, b, h, :], in_=banks[b][:, h * D:(h + 1) * D], func=ACT.Square, accum_out=ss[:, b, h:h + 1])
+                    nc.scalar.activation(out=sq[:, b, h, :], in_=banks[b][:, h * D:(h + 1) * D], func=ACT.Square, accum_out=ss[:, b, h:h + 1])
             st["ss", s] = ss
-            st["o", s] = o
 
         def root(s):
             if not 0 <= s < 16:
                 return
-            rinv = stage.tile([P, 2, 2, 4], F32, name="rinv", tag="rinv", bufs=4)
-            nc.scalar.activation(out=rinv[:], in_=st["ss", s][:].unsqueeze(2).to_broadcast([P, 2, 2, 4]), func=ACT.Abs_reciprocal_sqrt,
+            rinv = stage.tile([P, 2, 4], F32, name="rinv", tag="rinv", bufs=4)
+            nc.scalar.activation(out=rinv[:], in_=st["ss", s][:], func=ACT.Abs_reciprocal_sqrt,
                                  bias=eps[:, 0:1], scale=1.0 / D)
             st["rinv", s] = rinv
-
-        def tables(s):
-            if not 0 <= s < 16:
-                return
-            rtab = stage.tile([P, 16, NROT], F32, name="rtab", tag="rtab", bufs=3)
-            j = (2 * unit(s)[1]) % 4
-            nc.gpsimd.tensor_tensor(out=rtab[:].rearrange("p (a h) i -> p a h i", h=4),
-                                    in0=tab[:, j:j + 2, :, :].rearrange("p b c i -> p (b c) i").unsqueeze(2).to_broadcast([P, 4, 4, NROT]),
-                                    in1=st["rinv", s][:].rearrange("p b c h -> p (b c) h").unsqueeze(3).to_broadcast([P, 4, 4, NROT]), op=ALU.mult)
-            st["rtab", s] = rtab
 
         def unrotated(s):
             if not 0 <= s < 16:
@@ -246,18 +236,21 @@ def tile_causalselfattention_pa_kernel(tc, x, ve, qkv_w_bytes, qkv_w_scale, lamb
                 for h in range(4):
                     nc.scalar.activation(out=st["o", s][:, b, h, :].rearrange("p (w d) -> p w d", w=2)[:, :, NROT:64],
                                          in_=banks[b][:, h * D:(h + 1) * D].rearrange("p (w d) -> p w d", w=2)[:, :, NROT:64],
-                                         func=ACT.Copy, scale=st["rinv", s][:, b, 0, h:h + 1])
+                                         func=ACT.Copy, scale=st["rinv", s][:, b, h:h + 1])
 
         def products(s):
             if not 0 <= s < 16:
                 return
             banks = banks_of(s)
             rab = stage.tile([P, 2, 2, 8, NROT], F32, name="rab", tag="rab", bufs=3)
+            j = (2 * unit(s)[1]) % 4
             for b in range(2):
                 nc.vector.tensor_tensor(out=rab[:, b, :, :, :],
                                         in0=banks[b][:].rearrange("p (m d) -> p m d", d=64)[:, :, 0:NROT].unsqueeze(1).to_broadcast([P, 2, 8, NROT]),
-                                        in1=st["rtab", s][:, 8 * b:8 * b + 8, :].unsqueeze(2).to_broadcast([P, 8, 2, NROT]), op=ALU.mult)
+                                        in1=tab[:, j + b, :, :].unsqueeze(2).to_broadcast([P, 2, 8, NROT]), op=ALU.mult)
             st["rab", s] = rab
+            o = stage.tile([P, 2, 4, D], F32, name="o", tag="o", bufs=6)
+            st["o", s] = o
 
         def adds(s):
             if not 0 <= s < 16:
@@ -267,6 +260,19 @@ def tile_causalselfattention_pa_kernel(tc, x, ve, qkv_w_bytes, qkv_w_scale, lamb
             eng = nc.vector if s in VADD else nc.gpsimd
             eng.tensor_tensor(out=o6[:, :, 0, 0:NROT], in0=r6[:, :, 0, :, 0, :], in1=r6[:, :, 1, :, 1, :], op=ALU.add)
             eng.tensor_tensor(out=o6[:, :, 1, 0:NROT], in0=r6[:, :, 0, :, 1, :], in1=r6[:, :, 1, :, 0, :], op=ALU.subtract)
+
+        def rotated(s):
+            if not 0 <= s < 16:
+                return
+            if s in SROT:
+                for b in range(2):
+                    for hh in range(4):
+                        o3 = st["o", s][:, b, hh, :].rearrange("p (w d) -> p w d", w=2)[:, :, 0:NROT]
+                        nc.scalar.activation(out=o3, in_=o3, func=ACT.Copy, scale=st["rinv", s][:, b, hh:hh + 1])
+                return
+            o4 = st["o", s][:].rearrange("p b h (w d) -> p (b h) w d", w=2)[:, :, :, 0:NROT]
+            nc.gpsimd.tensor_tensor(out=o4, in0=o4, in1=st["rinv", s][:].rearrange("p b h -> p (b h)").unsqueeze(2).unsqueeze(3).to_broadcast([P, 8, 2, NROT]),
+                                    op=ALU.mult)
 
         def store(s):
             if not 0 <= s < 16:
@@ -366,26 +372,28 @@ def tile_causalselfattention_pa_kernel(tc, x, ve, qkv_w_bytes, qkv_w_scale, lamb
         x_turn(7)
         root_table()
         mm(0, 0)
+        mm(0, 1)
         mul(1)
         turn(2)
         x_quant(3)
+        mm(1, 0)
 
-        for s in range(-2, 18):
+        for s in range(0, 18):
             products(s)
-            mm(s + 2, 1)
-            mm(s + 3, 0)
-            tables(s + 1)
-            adds(s - 1)
-            squares(s + 2)
-            root(s + 2)
+            mm(s + 1, 1)
+            adds(s)
+            squares(s)
+            root(s)
+            mm(s + 2, 0)
             quant()
             mul(1)
             turn(1)
             cast(1)
+            unrotated(s)
+            rotated(s)
             if s >= V0:
                 vblend()
-            unrotated(s + 2)
-            if s % 2 == 0:
+            if s < 9:
                 mul(1)
                 turn(1)
                 cast(1)
@@ -393,6 +401,6 @@ def tile_causalselfattention_pa_kernel(tc, x, ve, qkv_w_bytes, qkv_w_scale, lamb
                 vblend()
             if s >= V0 - 1:
                 vahead()
-            store(s - 1)
+            store(s)
             if s >= 3:
                 vescale(1)

@@ -25,7 +25,9 @@ EPS = 2.0 ** -23
 RATIO = (1.0 / 1024.0) ** (1.0 / 31.0)
 HEADRUNS = 12
 NWARM = 4
-VADD = (13, 14, 15)
+VADD = (14, 15)
+GVE = (0, 1, 2, 3)
+VEND = 2
 V0 = 8
 ACC, TP, VB = 5, 2, 1
 SROT = ()
@@ -282,7 +284,10 @@ def tile_causalselfattention_pa_kernel(tc, x, ve, qkv_w_bytes, qkv_w_scale, lamb
                               in_=st["o", s][:].rearrange("p b h d -> p b (h d)"))
 
         def ve_scale(tt):
-            nc.scalar.activation(out=ve1[tt][:], in_=veraw[tt // 2][:, tt % 2, :], func=ACT.Copy, scale=lam[:, 1:2])
+            if tt in GVE:
+                nc.gpsimd.tensor_scalar(out=ve1[tt][:], in0=veraw[tt // 2][:, tt % 2, :], scalar1=lam_bf[:, 1:2], scalar2=0.0, op0=ALU.mult, op1=ALU.add)
+            else:
+                nc.scalar.activation(out=ve1[tt][:], in_=veraw[tt // 2][:, tt % 2, :], func=ACT.Copy, scale=lam[:, 1:2])
 
         def vmm(n):
             spare = q["turn"] == 24 and n % 3 != 0
@@ -361,9 +366,9 @@ def tile_causalselfattention_pa_kernel(tc, x, ve, qkv_w_bytes, qkv_w_scale, lamb
         mul(1)
         x_quant(1)
         quant()
-        cast(6)
         x_turn(4)
         x_turn(5)
+        cast(6)
         turn(2)
         mul(1)
         x_quant(2)
@@ -378,7 +383,7 @@ def tile_causalselfattention_pa_kernel(tc, x, ve, qkv_w_bytes, qkv_w_scale, lamb
         x_quant(3)
         mm(1, 0)
 
-        for s in range(0, 18):
+        for s in range(16):
             products(s)
             mm(s + 1, 1)
             adds(s)
@@ -391,16 +396,20 @@ def tile_causalselfattention_pa_kernel(tc, x, ve, qkv_w_bytes, qkv_w_scale, lamb
             cast(1)
             unrotated(s)
             rotated(s)
-            if s >= V0:
+            if s >= V0 and q["v"] < 16 - VEND:
                 vblend()
             if s < 9:
                 mul(1)
                 turn(1)
                 cast(1)
-            if s >= V0:
+            if s >= V0 and q["v"] < 16 - VEND:
                 vblend()
             if s >= V0 - 1:
                 vahead()
-            store(s)
+            store(s - 1)
             if s >= 3:
                 vescale(1)
+        for n in range(VEND):
+            vblend()
+            if n == 1:
+                store(15)

from contextlib import ExitStack
import math

import concourse.masks as masks
import concourse.mybir as mybir

F32 = mybir.dt.float32
BF16 = mybir.dt.bfloat16
I32 = mybir.dt.int32
U32 = mybir.dt.uint32
U8 = mybir.dt.uint8
FP8 = mybir.dt.float8_e4m3fn
FP8X4 = mybir.dt.float8_e4m3fn_x4
ALU = mybir.AluOpType
ACT = mybir.ActivationFunctionType

P = 128
TOK = 1024
C = 1024
HEADS = 8
D = 128
NROT = 32
FLOPS = 2 * TOK * C * 3 * HEADS * D
EPS = 2.0 ** -23
RATIO = (1.0 / 1024.0) ** (1.0 / 31.0)
HEADRUNS = 12
NWARM = 4
VADD = (14, 15)
GVE = (0, 1, 2, 3)
VEND = 2
V0 = 8
ACC, TP, VB = 5, 2, 1
SROT = ()
VCAST = (0, 1)
SCAST = (2, 3, 5, 7) + tuple(range(9, 24))


def tile_causalselfattention_pa_kernel(tc, x, ve, qkv_w_bytes, qkv_w_scale, lambdas, out_0, out_1, out_2):
    nc = tc.nc
    xf = x.flatten_outer_dims().rearrange("(n p) k -> p n k", p=P)
    vef = ve.flatten_outer_dims().rearrange("(n p) k -> p n k", p=P)
    wv = qkv_w_bytes.rearrange("s n k -> (s n) k").rearrange("(c r p) k -> p c r k", r=4, p=P)
    outs = [o.rearrange("b t h d -> (b t) (h d)").rearrange("(n p) c -> p n c", p=P) for o in (out_0, out_1, out_2)]

    with ExitStack() as ctx:
        const = ctx.enter_context(tc.tile_pool(name="const", bufs=1))
        keep = ctx.enter_context(tc.tile_pool(name="keep", bufs=1))
        stage = ctx.enter_context(tc.tile_pool(name="stage", bufs=2))
        psum = ctx.enter_context(tc.psum_pool(name="psum", bufs=2))
        ctx.enter_context(tc.manual_schedule())

        sck = const.tile([P, 2, 4], F32, name="sck")
        nc.scalar.dma_start(out=sck[:], in_=qkv_w_scale.rearrange("a b (g p t) -> p (a b g) t", p=P, t=4))
        lam_bf = const.tile([P, 2], BF16, name="lam_bf")
        nc.scalar.dma_start(out=lam_bf[:], in_=lambdas.partition_broadcast(P))
        wbytes = [keep.tile([P, 4, C], U8, name="wbytes%d" % c) for c in range(6)]
        xraw = [keep.tile([P, 2, C], BF16, name="xraw%d" % i) for i in range(4)]
        veraw = [keep.tile([P, 2, C], BF16, name="veraw%d" % i) for i in range(4)]

        def load_w(c):
            nc.sync.dma_start(out=wbytes[c][:], in_=wv[:, c, :, :])

        def load_x(i):
            nc.sync.dma_start(out=xraw[i][:], in_=xf[:, 2 * i:2 * i + 2, :])

        def load_ve(i):
            nc.sync.dma_start(out=veraw[i][:], in_=vef[:, 2 * i:2 * i + 2, :])

        for r in range(4):
            nc.sync.dma_start(out=wbytes[0][:, r, :], in_=wv[:, 0, r, :])
        for i in range(2):
            nc.sync.dma_start(out=xraw[0][:, i, :], in_=xf[:, i, :])
        load_x(1)
        load_w(1)
        load_x(2)
        load_x(3)
        load_ve(0)
        load_w(2)
        load_ve(1)
        load_w(3)
        load_w(4)
        load_ve(2)
        load_ve(3)
        load_w(5)

        zeros = const.tile([P, 512], BF16, name="zeros")
        nc.vector.memset(zeros[:], 0.0)
        tpos = const.tile([P, 4], F32, name="tpos")
        nc.gpsimd.iota(tpos[:], pattern=[[P, 4]], base=0, channel_multiplier=1, allow_small_or_imprecise_dtypes=True)
        ident = const.tile([P, P], F32, name="ident")
        masks.make_identity(nc, ident[:])
        eps = const.tile([P, 1], F32, name="eps")
        nc.gpsimd.memset(eps[:], EPS)
        turns = const.tile([P, 2, 4, NROT], F32, name="turns")
        nc.vector.tensor_scalar(out=turns[:, 0, :, 0], in0=tpos[:], scalar1=1.0 / (2.0 * math.pi), scalar2=None, op0=ALU.mult)
        for n in (1, 2, 4, 8, 16):
            nc.vector.tensor_scalar(out=turns[:, 0, :, n:2 * n], in0=turns[:, 0, :, 0:n], scalar1=RATIO ** n, scalar2=None, op0=ALU.mult)
        turns_flat = turns[:].rearrange("p a j i -> p (a j i)")
        whole_i = const.tile([P, 8 * NROT], I32, name="whole_i")
        frac = const.tile([P, 8 * NROT], F32, name="frac")
        negfrac = const.tile([P, 8 * NROT], F32, name="negfrac")

        def quarter_turn():
            nc.vector.tensor_scalar(out=turns[:, 1, :, :], in0=turns[:, 0, :, :], scalar1=0.25, scalar2=None, op0=ALU.add)

        def whole_turns():
            nc.vector.tensor_copy(out=whole_i[:], in_=turns_flat)

        def fractions():
            nc.vector.tensor_tensor(out=frac[:], in0=turns_flat, in1=whole_i[:], op=ALU.subtract)

        def half_turns():
            nc.vector.scalar_tensor_tensor(out=negfrac[:], in0=frac[:], scalar=0.5, in1=frac[:], op0=ALU.is_gt, op1=ALU.subtract)

        tab = const.tile([P, 4, 2, NROT], F32, name="tab")
        lam = const.tile([P, 2], F32, name="lam")
        nc.gpsimd.tensor_copy(out=lam[:], in_=lam_bf[:])

        xc = [keep.tile([P, 512], U32, name="xc%d" % m, align_bytes=64) for m in range(4)]
        xs = [keep.tile([P, 512], U8, name="xs%d" % m, align_bytes=64) for m in range(4)]
        wc = [keep.tile([P, 1024], U32, name="wc%d" % c, align_bytes=64) for c in range(6)]
        ws = [keep.tile([P, 1024], U8, name="ws%d" % c, align_bytes=64) for c in range(6)]
        ve1 = [keep.tile([P, C], F32, name="ve1_%d" % i) for i in range(8)]
        st = {}

        warmbank = psum.tile([P, 512], F32, name="tp", tag="tp", bufs=TP)
        for k in range(NWARM):
            nc.tensor.matmul(out=warmbank[:], lhsT=zeros[:, 0:P], rhs=zeros[:], start=True, stop=True)
        warm = const.tile([P, 1], F32, name="warm")

        def sines():
            for a in range(2):
                nc.scalar.activation(out=tab[:, :, 1 - a, :], in_=negfrac[:].rearrange("p (a j i) -> p a j i", a=2, j=4)[:, a, :, :],
                                     func=ACT.Sin, scale=-2.0 * math.pi)

        def root_table():
            nc.scalar.activation(out=warm[:], in_=eps[:], func=ACT.Abs_reciprocal_sqrt)

        def bank_for_run():
            r = st["runs"] = st.get("runs", -1) + 1
            if r < HEADRUNS and r % 8 < ACC:
                return psum.tile([P, 2, 2, P], F32, name="acc", tag="acc", bufs=ACC)
            if r < HEADRUNS and r % 8 < ACC + VB:
                return psum.tile([P, 2, 2, P], F32, name="vac", tag="vac", bufs=VB)
            return psum.tile([P, 2, 2, P], F32, name="tp", tag="tp", bufs=TP)

        def transposes(key, words):
            tp = bank_for_run()
            for u in range(2):
                for g in range(2):
                    nc.tensor.transpose(tp[:, u, g, :], words[:, 256 * g + u:256 * (g + 1):2], ident[:])
            st[key] = tp

        def x_turn(i):
            transposes(("xt", i), xraw[i // 2][:, i % 2, :].bitcast(F32))
            if i % 2 == 0:
                st["xg", i // 2] = stage.tile([P, 2, 256, 2], F32, name="xg", tag="xg", bufs=3, align_bytes=64)
            nc.scalar.copy(out=st["xg", i // 2][:, i % 2, :, :], in_=st["xt", i][:].rearrange("p u g r -> p (g r) u"))

        def x_quant(m):
            nc.vector.quantize_mx(out=xc[m][:].bitcast(FP8X4), scales=xs[m][:],
                                  in_=st["xg", m][:].rearrange("p i r u -> p (i r u)").bitcast(BF16))

        def w_cast(rt):
            wb = stage.tile([P, C], BF16, name="wb", tag="wb", bufs=10)
            src = wbytes[rt // 4][:, rt % 4, :].bitcast(FP8)
            if rt in VCAST:
                nc.vector.tensor_copy(out=wb[:], in_=src)
            elif rt in SCAST:
                nc.scalar.copy(out=wb[:], in_=src)
            else:
                nc.gpsimd.tensor_copy(out=wb[:], in_=src)
            st["wb", rt] = wb

        def w_transpose(rt):
            transposes(("wt", rt), st["wb", rt][:].bitcast(F32))

        def w_mul(rt):
            c, r = divmod(rt, 4)
            if r == 0:
                st["wg", c] = stage.tile([P, 2, 4, 512], BF16, name="wg", tag="wg", bufs=2, align_bytes=64)
            nc.vector.tensor_tensor(out=st["wg", c][:, :, r, :],
                                    in0=st["wt", rt][:].bitcast(BF16).rearrange("p u g (r e) -> p (g r) u e", e=2),
                                    in1=sck[:].unsqueeze(2).to_broadcast([P, 2, P, 4]), op=ALU.mult)

        def w_quant(c):
            nc.vector.quantize_mx(out=wc[c][:].bitcast(FP8X4), scales=ws[c][:],
                                  in_=st["wg", c][:].rearrange("p g r m -> p (g r m)"))

        def project(c, tt, tag, bufs):
            acc = psum.tile([P, 512], F32, name=tag, tag=tag, bufs=bufs)
            for g in range(2):
                rows = slice((2 * (tt % 2) + g) * P, (2 * (tt % 2) + g + 1) * P)
                nc.tensor.matmul_mx(out=acc[:],
                                    lhsT=xc[tt // 2][:, rows].bitcast(FP8X4),
                                    lhsT_scale=xs[tt // 2][:, rows],
                                    rhs=wc[c][:, g * 512:(g + 1) * 512].bitcast(FP8X4),
                                    rhs_scale=ws[c][:, g * 512:(g + 1) * 512],
                                    start=(g == 0), stop=(g == 1))
            return acc

        def unit(s):
            return s // 4, s % 4

        def mm(s, half):
            c, m = unit(s)
            if s < 16:
                st["acc", c, m, half] = project(c, 2 * m + half, "acc", ACC)

        def banks_of(s):
            c, m = unit(s)
            return [st["acc", c, m, half] for half in range(2)]

        def squares(s):
            if not 0 <= s < 16:
                return
            banks = banks_of(s)
            ss = stage.tile([P, 2, 4], F32, name="ss", tag="ss", bufs=4)
            sq = stage.tile([P, 2, 4, D], BF16, name="sq", tag="sq", bufs=2)
            for b in range(2):
                for h in range(4):
                    nc.scalar.activation(out=sq[:, b, h, :], in_=banks[b][:, h * D:(h + 1) * D], func=ACT.Square, accum_out=ss[:, b, h:h + 1])
            st["ss", s] = ss

        def root(s):
            if not 0 <= s < 16:
                return
            rinv = stage.tile([P, 2, 4], F32, name="rinv", tag="rinv", bufs=4)
            nc.scalar.activation(out=rinv[:], in_=st["ss", s][:], func=ACT.Abs_reciprocal_sqrt,
                                 bias=eps[:, 0:1], scale=1.0 / D)
            st["rinv", s] = rinv

        def unrotated(s):
            if not 0 <= s < 16:
                return
            banks = banks_of(s)
            for b in range(2):
                for h in range(4):
                    nc.scalar.activation(out=st["o", s][:, b, h, :].rearrange("p (w d) -> p w d", w=2)[:, :, NROT:64],
                                         in_=banks[b][:, h * D:(h + 1) * D].rearrange("p (w d) -> p w d", w=2)[:, :, NROT:64],
                                         func=ACT.Copy, scale=st["rinv", s][:, b, h:h + 1])

        def products(s):
            if not 0 <= s < 16:
                return
            banks = banks_of(s)
            rab = stage.tile([P, 2, 2, 8, NROT], F32, name="rab", tag="rab", bufs=3)
            j = (2 * unit(s)[1]) % 4
            for b in range(2):
                nc.vector.tensor_tensor(out=rab[:, b, :, :, :],
                                        in0=banks[b][:].rearrange("p (m d) -> p m d", d=64)[:, :, 0:NROT].unsqueeze(1).to_broadcast([P, 2, 8, NROT]),
                                        in1=tab[:, j + b, :, :].unsqueeze(2).to_broadcast([P, 2, 8, NROT]), op=ALU.mult)
            st["rab", s] = rab
            o = stage.tile([P, 2, 4, D], F32, name="o", tag="o", bufs=6)
            st["o", s] = o

        def adds(s):
            if not 0 <= s < 16:
                return
            r6 = st["rab", s][:].rearrange("p b c (h w) i -> p b c h w i", w=2)
            o6 = st["o", s][:].rearrange("p b h (w d) -> p (b h) w d", w=2)
            eng = nc.vector if s in VADD else nc.gpsimd
            eng.tensor_tensor(out=o6[:, :, 0, 0:NROT], in0=r6[:, :, 0, :, 0, :], in1=r6[:, :, 1, :, 1, :], op=ALU.add)
            eng.tensor_tensor(out=o6[:, :, 1, 0:NROT], in0=r6[:, :, 0, :, 1, :], in1=r6[:, :, 1, :, 0, :], op=ALU.subtract)

        def rotated(s):
            if not 0 <= s < 16:
                return
            if s in SROT:
                for b in range(2):
                    for hh in range(4):
                        o3 = st["o", s][:, b, hh, :].rearrange("p (w d) -> p w d", w=2)[:, :, 0:NROT]
                        nc.scalar.activation(out=o3, in_=o3, func=ACT.Copy, scale=st["rinv", s][:, b, hh:hh + 1])
                return
            o4 = st["o", s][:].rearrange("p b h (w d) -> p (b h) w d", w=2)[:, :, :, 0:NROT]
            nc.gpsimd.tensor_tensor(out=o4, in0=o4, in1=st["rinv", s][:].rearrange("p b h -> p (b h)").unsqueeze(2).unsqueeze(3).to_broadcast([P, 8, 2, NROT]),
                                    op=ALU.mult)

        def store(s):
            if not 0 <= s < 16:
                return
            c, m = unit(s)
            nc.sync.dma_start(out=outs[c // 2][:, 2 * m:2 * m + 2, (c % 2) * 512:(c % 2 + 1) * 512],
                              in_=st["o", s][:].rearrange("p b h d -> p b (h d)"))

        def ve_scale(tt):
            if tt in GVE:
                nc.gpsimd.tensor_scalar(out=ve1[tt][:], in0=veraw[tt // 2][:, tt % 2, :], scalar1=lam_bf[:, 1:2], scalar2=0.0, op0=ALU.mult, op1=ALU.add)
            else:
                nc.scalar.activation(out=ve1[tt][:], in_=veraw[tt // 2][:, tt % 2, :], func=ACT.Copy, scale=lam[:, 1:2])

        def vmm(n):
            spare = q["turn"] == 24 and n % 3 != 0
            st["v", n] = project(4 + n // 8, n % 8, "tp" if spare else "vac", TP if spare else VB)

        def blend(n):
            ov = stage.tile([P, 512], F32, name="ov", tag="ov", bufs=6)
            cols = slice(n // 8 * 512, (n // 8 + 1) * 512)
            nc.vector.scalar_tensor_tensor(out=ov[:], in0=st["v", n][:], scalar=lam[:, 0:1],
                                           in1=ve1[n % 8][:, cols], op0=ALU.mult, op1=ALU.add)
            nc.sync.dma_start(out=outs[2][:, n % 8, cols], in_=ov[:])

        q = {"cast": 0, "turn": 0, "mul": 0, "z": 0, "ve": 0, "v": 0, "vm": 0}

        def cast(n):
            for k in range(n):
                if q["cast"] < 24:
                    w_cast(q["cast"])
                    q["cast"] += 1

        def turn(n):
            for k in range(n):
                if q["turn"] < q["cast"]:
                    w_transpose(q["turn"])
                    q["turn"] += 1

        def mul(n):
            for k in range(n):
                if q["mul"] < q["turn"]:
                    w_mul(q["mul"])
                    q["mul"] += 1

        def quant():
            if q["z"] < 6 and q["mul"] >= 4 * q["z"] + 4:
                w_quant(q["z"])
                q["z"] += 1

        def vahead():
            while q["vm"] < min(16, 8 if q["z"] < 6 else 16, q["v"] + (3 if q["turn"] == 24 else 1)):
                vmm(q["vm"])
                q["vm"] += 1

        def vblend():
            if q["v"] < q["vm"]:
                blend(q["v"])
                q["v"] += 1
                vahead()

        def vescale(n):
            for k in range(n):
                if q["ve"] < 8:
                    ve_scale(q["ve"])
                    q["ve"] += 1

        quarter_turn()
        cast(1)
        whole_turns()
        cast(1)
        fractions()
        turn(1)
        cast(1)
        turn(1)
        cast(1)
        x_turn(0)
        x_turn(1)
        turn(1)
        mul(1)
        half_turns()
        turn(1)
        mul(1)
        x_turn(2)
        x_turn(3)
        sines()
        mul(1)
        x_quant(0)
        mul(1)
        x_quant(1)
        quant()
        x_turn(4)
        x_turn(5)
        cast(6)
        turn(2)
        mul(1)
        x_quant(2)
        vescale(1)
        x_turn(6)
        x_turn(7)
        root_table()
        mm(0, 0)
        mm(0, 1)
        mul(1)
        turn(2)
        x_quant(3)
        mm(1, 0)

        for s in range(16):
            products(s)
            mm(s + 1, 1)
            adds(s)
            squares(s)
            root(s)
            mm(s + 2, 0)
            quant()
            mul(1)
            turn(1)
            cast(1)
            unrotated(s)
            rotated(s)
            if s >= V0 and q["v"] < 16 - VEND:
                vblend()
            if s < 9:
                mul(1)
                turn(1)
                cast(1)
            if s >= V0 and q["v"] < 16 - VEND:
                vblend()
            if s >= V0 - 1:
                vahead()
            store(s - 1)
            if s >= 3:
                vescale(1)
        for n in range(VEND):
            vblend()
            if n == 1:
                store(15)
